import numpy as np
import ml_dtypes


def mxq(x, axis, fmt="e4m3"):
    dtype, down = {"e4m3": (ml_dtypes.float8_e4m3fn, 7), "e5m2": (ml_dtypes.float8_e5m2, 14)}[fmt]
    v = np.moveaxis(np.asarray(x, np.float32).astype(ml_dtypes.bfloat16).astype(np.float64), axis, -1)
    blocks = v.reshape(v.shape[:-1] + (-1, 32))
    amax = np.abs(blocks).max(-1, keepdims=True)
    byte = np.maximum(np.where(amax > 0, np.frexp(amax)[1] - 1 + 127, 0) - down, 1)
    scale = np.exp2(byte - 127.0)
    codes = (blocks / scale).astype(np.float32).astype(dtype).astype(np.float64)
    return np.moveaxis((codes * scale).reshape(v.shape), -1, axis)


WIDE = False


def mx_kscale(k):
    if not WIDE:
        return np.ones(k)
    levels = np.array([10, -10, 5, -5, 0])
    a = np.random.permutation(np.resize(levels, k // 512 * 4)).reshape(k // 512, 4)
    idx = np.arange(k)
    return np.exp2(a[idx // 512, idx % 128 // 32])


BF16 = ml_dtypes.bfloat16


def bf(x):
    return np.asarray(x, np.float32).astype(BF16)


def f64(x):
    return np.asarray(x).astype(np.float64)


N, C, P, D = 512, 128, 7, 1024
SCALE = 1.0 / np.sqrt(D)


def setup_inputs():
    t = mx_kscale(D)
    t = t / t.max()
    return {"q": bf(np.random.standard_normal((N, D)) * 1.6),
            "k": bf(np.random.standard_normal((N, D)) * 1.6),
            "feat": bf(np.random.standard_normal((N, D)) * t),
            "conv_w": bf(np.random.standard_normal((D, D)) * 2.0 / np.sqrt(D) / t),
            "conv_b": bf(np.random.standard_normal(D) * 0.1)}


def reference(q, k, feat, conv_w, conv_b):
    x = f64(feat)
    s = (f64(q) @ f64(k).T) * SCALE
    e = np.exp(s - s.max(-1, keepdims=True))
    agg = (mxq(e, 1, "e4m3") @ mxq(x, 0, "e4m3")) / e.sum(-1, keepdims=True)
    r = (mxq(agg, 1, "e4m3") @ mxq(f64(conv_w).T, 0, "e4m3")) + f64(conv_b)
    return np.maximum(x + r, 0.0)

@@ -1,0 +1,296 @@
+from contextlib import ExitStack
+
+import concourse.mybir as mybir
+from concourse.masks import make_identity
+
+F32 = mybir.dt.float32
+BF16 = mybir.dt.bfloat16
+U32 = mybir.dt.uint32
+U8 = mybir.dt.uint8
+FP8X4 = mybir.dt.float8_e4m3fn_x4
+ALU = mybir.AluOpType
+ACT = mybir.ActivationFunctionType
+AXIS = mybir.AxisListType
+
+P = 128
+PACK = 4
+N_PROP = 512
+D = 1024
+CHUNKS = N_PROP // P
+W_ROWS = D // P
+BANK = 512
+HALVES = D // BANK
+PASSES = D // (P * PACK)
+BLOCKS = D // (2 * P)
+SCALE = 1.0 / 32.0
+
+FLOPS = 2 * N_PROP * N_PROP * D * 2 + 2 * N_PROP * D * D
+
+
+def tile_selsahead_pa_kernel(tc, q, k, feat, conv_w, conv_b, out):
+    nc = tc.nc
+    with ExitStack() as ctx:
+        keep = ctx.enter_context(tc.tile_pool(name="keep", bufs=1))
+        work = ctx.enter_context(tc.tile_pool(name="work", bufs=2))
+        results = ctx.enter_context(tc.tile_pool(name="results", bufs=CHUNKS))
+        psum_bank = ctx.enter_context(tc.psum_pool(name="psum_bank", bufs=5))
+        psum_small = ctx.enter_context(tc.psum_pool(name="psum_small", bufs=1))
+        psum_agg = ctx.enter_context(tc.psum_pool(name="psum_agg", bufs=2))
+
+        q_view = q.rearrange("(p j) d -> p j d", j=CHUNKS)
+        k_view = k.rearrange("(p j) d -> p j d", j=CHUNKS)
+        feat_view = feat.rearrange("(p j) d -> p j d", j=CHUNKS)
+        out_view = out.rearrange("(p j) d -> p j d", j=CHUNKS)
+        w_view = conv_w.rearrange("(r p) d -> p r d", p=P)
+
+        q_sb = keep.tile([P, CHUNKS, D], BF16)
+        k_sb = keep.tile([P, CHUNKS, D], BF16)
+        feat_sb = keep.tile([P, CHUNKS, D], BF16)
+        w_sb = keep.tile([P, W_ROWS, D], BF16)
+        bias_rows = keep.tile([P, D], BF16)
+
+        nc.vector.memset(bias_rows[:], 0.0)
+        nc.scalar.dma_start(out=bias_rows[0:1, :], in_=conv_b.rearrange("(o d) -> o d", o=1))
+        nc.sync.dma_start(out=q_sb[:, 0, :], in_=q_view[:, 0, :])
+        nc.sync.dma_start(out=k_sb[:, 0:2, :], in_=k_view[:, 0:2, :])
+        nc.sync.dma_start(out=k_sb[:, 2:4, :], in_=k_view[:, 2:4, :])
+        nc.sync.dma_start(out=q_sb[:, 1, :], in_=q_view[:, 1, :])
+        nc.sync.dma_start(out=feat_sb[:], in_=feat_view)
+        nc.sync.dma_start(out=q_sb[:, 2:4, :], in_=q_view[:, 2:4, :])
+        for r in range(0, W_ROWS, 2):
+            nc.sync.dma_start(out=w_sb[:, r : r + 2, :], in_=w_view[:, r : r + 2, :])
+
+        ident_f32 = keep.tile([P, P], F32)
+        make_identity(nc, ident_f32[:])
+        ident_bf16 = keep.tile([P, P], BF16)
+        make_identity(nc, ident_bf16[:])
+        ones_bf16 = keep.tile([P, P], BF16)
+        nc.vector.memset(ones_bf16[:], 1.0)
+
+        q_t = keep.tile([P, CHUNKS, BLOCKS, P], F32)
+        k_t = keep.tile([P, BLOCKS, N_PROP], F32)
+        bias_all = keep.tile([P, D], BF16)
+        feat_bias = keep.tile([P, CHUNKS, D], F32)
+        feat_grouped = keep.tile([P, D, PACK], BF16, align_bytes=64)
+        feat_codes = keep.tile([P, D], U32, align_bytes=64)
+        feat_scales = keep.tile([P, D], U8, align_bytes=64)
+        w_grouped = keep.tile([P, PASSES, D, 2], F32, align_bytes=64)
+        w_codes = keep.tile([P, PASSES, D], U32, align_bytes=64)
+        w_scales = keep.tile([P, PASSES, D], U8, align_bytes=64)
+        e_codes = keep.tile([P, CHUNKS, P], U32, align_bytes=64)
+        e_scales = keep.tile([P, CHUNKS, P], U8, align_bytes=64)
+        agg_codes = keep.tile([P, CHUNKS, PASSES, P], U32, align_bytes=64)
+        agg_scales = keep.tile([P, CHUNKS, PASSES, P], U8, align_bytes=64)
+
+        for h in range(HALVES):
+            cols = slice(h * BANK, (h + 1) * BANK)
+            bias_ps = psum_bank.tile([P, BANK], F32, tag="bank")
+            nc.tensor.matmul(bias_ps[:], lhsT=ones_bf16[:], rhs=bias_rows[:, cols], start=True, stop=True)
+            nc.scalar.copy(out=bias_all[:, cols], in_=bias_ps[:])
+
+        def rows_job(rows, dest, copy):
+            words = rows.bitcast(F32)
+            sources = [words[:, c * P : (c + 1) * P] for c in range(BLOCKS)]
+            return sources, lambda bank: copy(out=dest, in_=bank[:])
+
+        def w_job(pair, g, copy):
+            sources = [
+                w_sb[:, 2 * pair + r, :].bitcast(F32)[:, (2 * g + u) * P : (2 * g + u + 1) * P]
+                for u in range(2)
+                for r in range(2)
+            ]
+            dest = w_grouped[:, g, 2 * pair * P : 2 * (pair + 1) * P, :]
+            return sources, lambda bank: copy(
+                out=dest, in_=bank[:].rearrange("w (u r) c -> w (r c) u", u=2)
+            )
+
+        def fill_bank(job):
+            sources, empty = job
+            bank = psum_bank.tile([P, 4, P], F32, tag="bank", name="t_bank")
+            for slot in range(4):
+                nc.tensor.transpose(bank[:, slot, :], sources[slot], ident_f32[:])
+            empty(bank)
+
+        def score_matmul(s_ps, j, m):
+            c, i = divmod(m, 2)
+            q_pairs = q_t[:, j, c, :].bitcast(BF16).rearrange("w (n i) -> w n i", i=2)
+            k_pairs = k_t[:, c, :].bitcast(BF16).rearrange("w (n i) -> w n i", i=2)
+            nc.tensor.matmul(
+                s_ps[:],
+                lhsT=q_pairs[:, :, i],
+                rhs=k_pairs[:, :, i],
+                start=(m == 0),
+                stop=(m == 2 * BLOCKS - 1),
+            )
+
+        def scores(j, jobs):
+            s_ps = psum_bank.tile([P, N_PROP], F32, tag="bank", name="s_ps")
+            if not jobs:
+                for m in range(2 * BLOCKS):
+                    score_matmul(s_ps, j, m)
+                return s_ps
+            matmuls_per_job = 2 * BLOCKS // len(jobs)
+            transposes_per_matmul = 4 // matmuls_per_job
+            for number, (sources, empty) in enumerate(jobs):
+                bank = psum_bank.tile([P, 4, P], F32, tag="bank", name="t_bank")
+                for step in range(matmuls_per_job):
+                    score_matmul(s_ps, j, number * matmuls_per_job + step)
+                    for slot in range(step * transposes_per_matmul, (step + 1) * transposes_per_matmul):
+                        nc.tensor.transpose(bank[:, slot, :], sources[slot], ident_f32[:])
+                empty(bank)
+            return s_ps
+
+        def softmax(s_ps):
+            row_max = work.tile([P, 1], F32)
+            nc.vector.reduce_max(out=row_max[:], in_=s_ps[:], axis=AXIS.X)
+            shift = work.tile([P, 1], F32)
+            nc.vector.tensor_scalar_mul(out=shift[:], in0=row_max[:], scalar1=-SCALE)
+            e_sb = work.tile([P, N_PROP], BF16)
+            row_sum = work.tile([P, 1], F32)
+            nc.scalar.activation(
+                out=e_sb[:], in_=s_ps[:], func=ACT.Exp, bias=shift[:], scale=SCALE, accum_out=row_sum[:]
+            )
+            return e_sb, row_sum
+
+        def quantise_e(j, e_sb, row_sum):
+            inv_sum = work.tile([P, 1], F32)
+            nc.vector.reciprocal(out=inv_sum[:], in_=row_sum[:])
+            small = psum_small.tile([P, BANK], F32)
+            e_t = small[:, 0 : BANK // 2].bitcast(BF16).rearrange("p (j n) -> p j n", j=CHUNKS)
+            for key_chunk in range(CHUNKS):
+                nc.tensor.transpose(
+                    e_t[:, key_chunk, :], e_sb[:, key_chunk * P : (key_chunk + 1) * P], ident_bf16[:]
+                )
+            inv_ps = small[:, BANK // 2 : BANK // 2 + P]
+            nc.tensor.matmul(
+                inv_ps, lhsT=inv_sum[:].to_broadcast([P, P]), rhs=ident_f32[:], start=True, stop=True
+            )
+            e_grouped = work.tile([P, P, PACK], BF16, align_bytes=64)
+            nc.scalar.copy(out=e_grouped[:], in_=e_t.rearrange("p j n -> p n j"))
+            inv_all = work.tile([P, P], F32)
+            nc.scalar.copy(out=inv_all[:], in_=inv_ps)
+            nc.vector.quantize_mx(
+                out=e_codes[:, j, :].bitcast(FP8X4),
+                scales=e_scales[:, j, :],
+                in_=e_grouped[:].rearrange("p n j -> p (n j)"),
+            )
+            return inv_all
+
+        def aggregate(j, inv_all):
+            agg_grouped = work.tile([P, PASSES, P, PACK], BF16, align_bytes=64)
+            for g in range(PASSES):
+                agg_ps = psum_agg.tile([P, PACK, P], F32)
+                for t in range(PACK):
+                    cols = slice((g * PACK + t) * P, (g * PACK + t + 1) * P)
+                    nc.tensor.matmul_mx(
+                        out=agg_ps[:, t, :],
+                        lhsT=feat_codes[:, cols].bitcast(FP8X4),
+                        lhsT_scale=feat_scales[:, cols],
+                        rhs=e_codes[:, j, :].bitcast(FP8X4),
+                        rhs_scale=e_scales[:, j, :],
+                        start=True,
+                        stop=True,
+                    )
+                nc.vector.tensor_tensor(
+                    out=agg_grouped[:, g, :, :],
+                    in0=agg_ps[:].rearrange("w t n -> w n t"),
+                    in1=inv_all[:].unsqueeze(2).to_broadcast([P, P, PACK]),
+                    op=ALU.mult,
+                )
+            nc.vector.quantize_mx(
+                out=agg_codes[:, j, :, :].rearrange("w g n -> w (g n)").bitcast(FP8X4),
+                scales=agg_scales[:, j, :, :].rearrange("w g n -> w (g n)"),
+                in_=agg_grouped[:].rearrange("w g n t -> w (g n t)"),
+            )
+
+        def project(j):
+            result = results.tile([P, D], F32)
+            for h in range(HALVES):
+                cols = slice(h * BANK, (h + 1) * BANK)
+                out_ps = psum_bank.tile([P, BANK], F32, tag="bank", name="out_ps")
+                for g in range(PASSES):
+                    nc.tensor.matmul_mx(
+                        out=out_ps[:],
+                        lhsT=agg_codes[:, j, g, :].bitcast(FP8X4),
+                        lhsT_scale=agg_scales[:, j, g, :],
+                        rhs=w_codes[:, g, cols].bitcast(FP8X4),
+                        rhs_scale=w_scales[:, g, cols],
+                        start=(g == 0),
+                        stop=(g == PASSES - 1),
+                    )
+                nc.vector.tensor_tensor(
+                    out=result[:, cols], in0=out_ps[:], in1=feat_bias[:, j, cols], op=ALU.add
+                )
+                if h == 0:
+                    nc.scalar.activation(out=result[:, cols], in_=result[:, cols], func=ACT.Relu)
+                else:
+                    nc.gpsimd.tensor_scalar(
+                        out=result[:, cols], in0=result[:, cols],
+                        scalar1=0.0, scalar2=0.0, op0=ALU.max, op1=ALU.add,
+                    )
+                nc.sync.dma_start(out=out_view[:, j, cols], in_=result[:, cols])
+
+        def prepare_feat():
+            sorted_src = feat_sb[:].rearrange("p j (a w i) -> p a i w j", a=BLOCKS, i=2)
+            sorted_dst = feat_grouped[:].rearrange("p (a i w) j -> p a i w j", a=BLOCKS, i=2)
+            for a in range(BLOCKS):
+                copy = nc.vector.tensor_copy if a % 2 == 0 else nc.scalar.copy
+                copy(out=sorted_dst[:, a], in_=sorted_src[:, a])
+            for g in range(PASSES):
+                cols = slice(g * BANK, (g + 1) * BANK)
+                nc.vector.quantize_mx(
+                    out=feat_codes[:, cols].bitcast(FP8X4),
+                    scales=feat_scales[:, cols],
+                    in_=feat_grouped[:, cols, :].rearrange("p c j -> p (c j)"),
+                )
+            for j in range(CHUNKS):
+                for h in range(HALVES):
+                    cols = slice(h * BANK, (h + 1) * BANK)
+                    nc.gpsimd.tensor_tensor(
+                        out=feat_bias[:, j, cols], in0=feat_sb[:, j, cols], in1=bias_all[:, cols], op=ALU.add
+                    )
+
+        def quantise_w(h):
+            cols = slice(h * BANK, (h + 1) * BANK)
+            for g in range(PASSES):
+                nc.vector.quantize_mx(
+                    out=w_codes[:, g, cols].bitcast(FP8X4),
+                    scales=w_scales[:, g, cols],
+                    in_=w_grouped[:, g, cols, :].rearrange("w c u -> w (c u)").bitcast(BF16),
+                )
+
+        vector_copy = nc.vector.tensor_copy
+        scalar_copy = nc.scalar.copy
+
+        def q_job(j, copy):
+            return rows_job(q_sb[:, j, :], q_t[:, j, :, :], copy)
+
+        fill_bank(q_job(0, vector_copy))
+        for j in range(CHUNKS):
+            copy = scalar_copy if j % 2 == 0 else vector_copy
+            fill_bank(rows_job(k_sb[:, j, :], k_t[:, :, j * P : (j + 1) * P], copy))
+        fill_bank(q_job(1, scalar_copy))
+        prepare_feat()
+
+        side_jobs = [
+            [],
+            [q_job(2, vector_copy), q_job(3, scalar_copy)],
+            [w_job(pair, g, vector_copy if g == 0 else scalar_copy) for pair in (0, 1) for g in range(PASSES)],
+            [w_job(pair, g, vector_copy if g == 0 else scalar_copy) for pair in (2, 3) for g in range(PASSES)],
+        ]
+
+        e_of = {}
+        inv_of = {}
+        for step in range(CHUNKS + 3):
+            if step < CHUNKS:
+                s_ps = scores(step, side_jobs[step])
+                e_of[step] = softmax(s_ps)
+                if step >= 2:
+                    quantise_w(step - 2)
+            if 0 <= step - 1 < CHUNKS:
+                e_sb, row_sum = e_of[step - 1]
+                inv_of[step - 1] = quantise_e(step - 1, e_sb, row_sum)
+            if 0 <= step - 2 < CHUNKS:
+                aggregate(step - 2, inv_of[step - 2])
+            if 0 <= step - 3 < CHUNKS:
+                project(step - 3)

@@ -30,6 +30,7 @@ FLOPS = 2 * N_PROP * N_PROP * D * 2 + 2 * N_PROP * D * D
 def tile_selsahead_pa_kernel(tc, q, k, feat, conv_w, conv_b, out):
     nc = tc.nc
     with ExitStack() as ctx:
+        ctx.enter_context(tc.manual_schedule())
         keep = ctx.enter_context(tc.tile_pool(name="keep", bufs=1))
         work = ctx.enter_context(tc.tile_pool(name="work", bufs=2))
         results = ctx.enter_context(tc.tile_pool(name="results", bufs=CHUNKS))
@@ -82,11 +83,18 @@ def tile_selsahead_pa_kernel(tc, q, k, feat, conv_w, conv_b, out):
         agg_codes = keep.tile([P, CHUNKS, PASSES, P], U32, align_bytes=64)
         agg_scales = keep.tile([P, CHUNKS, PASSES, P], U8, align_bytes=64)
 
-        for h in range(HALVES):
-            cols = slice(h * BANK, (h + 1) * BANK)
-            bias_ps = psum_bank.tile([P, BANK], F32, tag="bank")
-            nc.tensor.matmul(bias_ps[:], lhsT=ones_bf16[:], rhs=bias_rows[:, cols], start=True, stop=True)
-            nc.scalar.copy(out=bias_all[:, cols], in_=bias_ps[:])
+        def add_bias_to_feat():
+            for h in range(HALVES):
+                cols = slice(h * BANK, (h + 1) * BANK)
+                bias_ps = psum_bank.tile([P, BANK], F32, tag="bank")
+                nc.tensor.matmul(bias_ps[:], lhsT=ones_bf16[:], rhs=bias_rows[:, cols], start=True, stop=True)
+                nc.scalar.copy(out=bias_all[:, cols], in_=bias_ps[:])
+            for j in range(CHUNKS):
+                for h in range(HALVES):
+                    cols = slice(h * BANK, (h + 1) * BANK)
+                    nc.gpsimd.tensor_tensor(
+                        out=feat_bias[:, j, cols], in0=feat_sb[:, j, cols], in1=bias_all[:, cols], op=ALU.add
+                    )
 
         def rows_job(rows, dest, copy):
             words = rows.bitcast(F32)
@@ -152,9 +160,12 @@ def tile_selsahead_pa_kernel(tc, q, k, feat, conv_w, conv_b, out):
             )
             return e_sb, row_sum
 
-        def quantise_e(j, e_sb, row_sum):
+        def invert(row_sum):
             inv_sum = work.tile([P, 1], F32)
             nc.vector.reciprocal(out=inv_sum[:], in_=row_sum[:])
+            return inv_sum
+
+        def quantise_e(j, e_sb, inv_sum):
             small = psum_small.tile([P, BANK], F32)
             e_t = small[:, 0 : BANK // 2].bitcast(BF16).rearrange("p (j n) -> p j n", j=CHUNKS)
             for key_chunk in range(CHUNKS):
@@ -221,21 +232,17 @@ def tile_selsahead_pa_kernel(tc, q, k, feat, conv_w, conv_b, out):
                 nc.vector.tensor_tensor(
                     out=result[:, cols], in0=out_ps[:], in1=feat_bias[:, j, cols], op=ALU.add
                 )
-                if h == 0:
-                    nc.scalar.activation(out=result[:, cols], in_=result[:, cols], func=ACT.Relu)
-                else:
-                    nc.gpsimd.tensor_scalar(
-                        out=result[:, cols], in0=result[:, cols],
-                        scalar1=0.0, scalar2=0.0, op0=ALU.max, op1=ALU.add,
-                    )
+                nc.scalar.activation(out=result[:, cols], in_=result[:, cols], func=ACT.Relu)
                 nc.sync.dma_start(out=out_view[:, j, cols], in_=result[:, cols])
 
-        def prepare_feat():
+        def regroup_feat():
             sorted_src = feat_sb[:].rearrange("p j (a w i) -> p a i w j", a=BLOCKS, i=2)
             sorted_dst = feat_grouped[:].rearrange("p (a i w) j -> p a i w j", a=BLOCKS, i=2)
             for a in range(BLOCKS):
                 copy = nc.vector.tensor_copy if a % 2 == 0 else nc.scalar.copy
                 copy(out=sorted_dst[:, a], in_=sorted_src[:, a])
+
+        def quantise_feat():
             for g in range(PASSES):
                 cols = slice(g * BANK, (g + 1) * BANK)
                 nc.vector.quantize_mx(
@@ -243,12 +250,6 @@ def tile_selsahead_pa_kernel(tc, q, k, feat, conv_w, conv_b, out):
                     scales=feat_scales[:, cols],
                     in_=feat_grouped[:, cols, :].rearrange("p c j -> p (c j)"),
                 )
-            for j in range(CHUNKS):
-                for h in range(HALVES):
-                    cols = slice(h * BANK, (h + 1) * BANK)
-                    nc.gpsimd.tensor_tensor(
-                        out=feat_bias[:, j, cols], in0=feat_sb[:, j, cols], in1=bias_all[:, cols], op=ALU.add
-                    )
 
         def quantise_w(h):
             cols = slice(h * BANK, (h + 1) * BANK)
@@ -270,26 +271,32 @@ def tile_selsahead_pa_kernel(tc, q, k, feat, conv_w, conv_b, out):
             copy = scalar_copy if j % 2 == 0 else vector_copy
             fill_bank(rows_job(k_sb[:, j, :], k_t[:, :, j * P : (j + 1) * P], copy))
         fill_bank(q_job(1, scalar_copy))
-        prepare_feat()
+        regroup_feat()
 
         side_jobs = [
             [],
-            [q_job(2, vector_copy), q_job(3, scalar_copy)],
-            [w_job(pair, g, vector_copy if g == 0 else scalar_copy) for pair in (0, 1) for g in range(PASSES)],
-            [w_job(pair, g, vector_copy if g == 0 else scalar_copy) for pair in (2, 3) for g in range(PASSES)],
+            [q_job(2, scalar_copy), q_job(3, scalar_copy)] + [w_job(0, g, scalar_copy) for g in range(PASSES)],
+            [w_job(pair, g, scalar_copy) for pair in (1, 2) for g in range(PASSES)],
+            [w_job(3, g, scalar_copy) for g in range(PASSES)],
         ]
 
         e_of = {}
+        sum_of = {}
         inv_of = {}
         for step in range(CHUNKS + 3):
             if step < CHUNKS:
                 s_ps = scores(step, side_jobs[step])
-                e_of[step] = softmax(s_ps)
-                if step >= 2:
-                    quantise_w(step - 2)
             if 0 <= step - 1 < CHUNKS:
-                e_sb, row_sum = e_of[step - 1]
-                inv_of[step - 1] = quantise_e(step - 1, e_sb, row_sum)
+                inv_sum = invert(sum_of[step - 1])
+            if step < CHUNKS:
+                e_of[step], sum_of[step] = softmax(s_ps)
+            if step == 0:
+                quantise_feat()
+                add_bias_to_feat()
+            if step in (2, 3):
+                quantise_w(step - 2)
+            if 0 <= step - 1 < CHUNKS:
+                inv_of[step - 1] = quantise_e(step - 1, e_of[step - 1], inv_sum)
             if 0 <= step - 2 < CHUNKS:
                 aggregate(step - 2, inv_of[step - 2])
             if 0 <= step - 3 < CHUNKS:

@@ -1,3 +1,4 @@
+import math
 from contextlib import ExitStack
 
 import concourse.mybir as mybir
@@ -83,12 +84,14 @@ def tile_selsahead_pa_kernel(tc, q, k, feat, conv_w, conv_b, out):
         agg_codes = keep.tile([P, CHUNKS, PASSES, P], U32, align_bytes=64)
         agg_scales = keep.tile([P, CHUNKS, PASSES, P], U8, align_bytes=64)
 
-        def add_bias_to_feat():
+        def spread_bias():
             for h in range(HALVES):
                 cols = slice(h * BANK, (h + 1) * BANK)
                 bias_ps = psum_bank.tile([P, BANK], F32, tag="bank")
                 nc.tensor.matmul(bias_ps[:], lhsT=ones_bf16[:], rhs=bias_rows[:, cols], start=True, stop=True)
                 nc.scalar.copy(out=bias_all[:, cols], in_=bias_ps[:])
+
+        def add_bias_to_feat():
             for j in range(CHUNKS):
                 for h in range(HALVES):
                     cols = slice(h * BANK, (h + 1) * BANK)
@@ -148,11 +151,14 @@ def tile_selsahead_pa_kernel(tc, q, k, feat, conv_w, conv_b, out):
                 empty(bank)
             return s_ps
 
-        def softmax(s_ps):
+        def row_shift(s_ps):
             row_max = work.tile([P, 1], F32)
             nc.vector.reduce_max(out=row_max[:], in_=s_ps[:], axis=AXIS.X)
             shift = work.tile([P, 1], F32)
             nc.vector.tensor_scalar_mul(out=shift[:], in0=row_max[:], scalar1=-SCALE)
+            return shift
+
+        def exponentials(s_ps, shift):
             e_sb = work.tile([P, N_PROP], BF16)
             row_sum = work.tile([P, 1], F32)
             nc.scalar.activation(
@@ -165,27 +171,33 @@ def tile_selsahead_pa_kernel(tc, q, k, feat, conv_w, conv_b, out):
             nc.vector.reciprocal(out=inv_sum[:], in_=row_sum[:])
             return inv_sum
 
-        def quantise_e(j, e_sb, inv_sum):
+        def turn(e_sb, inv_sum):
             small = psum_small.tile([P, BANK], F32)
             e_t = small[:, 0 : BANK // 2].bitcast(BF16).rearrange("p (j n) -> p j n", j=CHUNKS)
-            for key_chunk in range(CHUNKS):
-                nc.tensor.transpose(
-                    e_t[:, key_chunk, :], e_sb[:, key_chunk * P : (key_chunk + 1) * P], ident_bf16[:]
-                )
             inv_ps = small[:, BANK // 2 : BANK // 2 + P]
-            nc.tensor.matmul(
-                inv_ps, lhsT=inv_sum[:].to_broadcast([P, P]), rhs=ident_f32[:], start=True, stop=True
-            )
-            e_grouped = work.tile([P, P, PACK], BF16, align_bytes=64)
-            nc.scalar.copy(out=e_grouped[:], in_=e_t.rearrange("p j n -> p n j"))
-            inv_all = work.tile([P, P], F32)
-            nc.scalar.copy(out=inv_all[:], in_=inv_ps)
+            e_grouped = None
+            inv_all = None
+            if e_sb is not None:
+                for key_chunk in range(CHUNKS):
+                    nc.tensor.transpose(
+                        e_t[:, key_chunk, :], e_sb[:, key_chunk * P : (key_chunk + 1) * P], ident_bf16[:]
+                    )
+            if inv_sum is not None:
+                nc.tensor.transpose(inv_ps, inv_sum[:].to_broadcast([P, P]), ident_f32[:])
+            if e_sb is not None:
+                e_grouped = work.tile([P, P, PACK], BF16, align_bytes=64)
+                nc.scalar.copy(out=e_grouped[:], in_=e_t.rearrange("p j n -> p n j"))
+            if inv_sum is not None:
+                inv_all = work.tile([P, P], F32)
+                nc.scalar.copy(out=inv_all[:], in_=inv_ps)
+            return e_grouped, inv_all
+
+        def quantise_e(j, e_grouped):
             nc.vector.quantize_mx(
                 out=e_codes[:, j, :].bitcast(FP8X4),
                 scales=e_scales[:, j, :],
                 in_=e_grouped[:].rearrange("p n j -> p (n j)"),
             )
-            return inv_all
 
         def aggregate(j, inv_all):
             agg_grouped = work.tile([P, PASSES, P, PACK], BF16, align_bytes=64)
@@ -208,6 +220,9 @@ def tile_selsahead_pa_kernel(tc, q, k, feat, conv_w, conv_b, out):
                     in1=inv_all[:].unsqueeze(2).to_broadcast([P, P, PACK]),
                     op=ALU.mult,
                 )
+            return agg_grouped
+
+        def quantise_agg(j, agg_grouped):
             nc.vector.quantize_mx(
                 out=agg_codes[:, j, :, :].rearrange("w g n -> w (g n)").bitcast(FP8X4),
                 scales=agg_scales[:, j, :, :].rearrange("w g n -> w (g n)"),
@@ -232,7 +247,9 @@ def tile_selsahead_pa_kernel(tc, q, k, feat, conv_w, conv_b, out):
                 nc.vector.tensor_tensor(
                     out=result[:, cols], in0=out_ps[:], in1=feat_bias[:, j, cols], op=ALU.add
                 )
-                nc.scalar.activation(out=result[:, cols], in_=result[:, cols], func=ACT.Relu)
+                nc.gpsimd.tensor_scalar(
+                    out=result[:, cols], in0=result[:, cols], scalar1=math.inf, scalar2=0.0, op0=ALU.min, op1=ALU.max
+                )
                 nc.sync.dma_start(out=out_view[:, j, cols], in_=result[:, cols])
 
         def regroup_feat():
@@ -266,38 +283,54 @@ def tile_selsahead_pa_kernel(tc, q, k, feat, conv_w, conv_b, out):
         def q_job(j, copy):
             return rows_job(q_sb[:, j, :], q_t[:, j, :, :], copy)
 
+        table_warmer = keep.tile([P, 1], F32)
+        nc.vector.memset(table_warmer[:], 0.0)
+        nc.scalar.activation(out=table_warmer[:], in_=table_warmer[:], func=ACT.Exp)
+
         fill_bank(q_job(0, vector_copy))
         for j in range(CHUNKS):
             copy = scalar_copy if j % 2 == 0 else vector_copy
             fill_bank(rows_job(k_sb[:, j, :], k_t[:, :, j * P : (j + 1) * P], copy))
         fill_bank(q_job(1, scalar_copy))
+        spread_bias()
         regroup_feat()
 
         side_jobs = [
             [],
-            [q_job(2, scalar_copy), q_job(3, scalar_copy)] + [w_job(0, g, scalar_copy) for g in range(PASSES)],
-            [w_job(pair, g, scalar_copy) for pair in (1, 2) for g in range(PASSES)],
+            [q_job(2, vector_copy), q_job(3, scalar_copy), w_job(0, 0, vector_copy), w_job(0, 1, scalar_copy)],
+            [w_job(pair, g, vector_copy if g == 0 else scalar_copy) for pair in (1, 2) for g in range(PASSES)],
             [w_job(3, g, scalar_copy) for g in range(PASSES)],
         ]
 
         e_of = {}
         sum_of = {}
         inv_of = {}
-        for step in range(CHUNKS + 3):
-            if step < CHUNKS:
-                s_ps = scores(step, side_jobs[step])
-            if 0 <= step - 1 < CHUNKS:
-                inv_sum = invert(sum_of[step - 1])
-            if step < CHUNKS:
-                e_of[step], sum_of[step] = softmax(s_ps)
-            if step == 0:
+        for r in range(CHUNKS + 3):
+            starting = r < CHUNKS
+            turning = 0 <= r - 1 < CHUNKS
+            aggregating = 0 <= r - 2 < CHUNKS
+            projecting = 0 <= r - 3 < CHUNKS
+            if starting:
+                s_ps = scores(r, side_jobs[r])
+                shift = row_shift(s_ps)
+            if turning or aggregating:
+                e_grouped, inv_all = turn(e_of.get(r - 1), inv_of.get(r - 2))
+            if starting:
+                e_of[r], sum_of[r] = exponentials(s_ps, shift)
+            if r == 0:
                 quantise_feat()
                 add_bias_to_feat()
-            if step in (2, 3):
-                quantise_w(step - 2)
-            if 0 <= step - 1 < CHUNKS:
-                inv_of[step - 1] = quantise_e(step - 1, e_of[step - 1], inv_sum)
-            if 0 <= step - 2 < CHUNKS:
-                aggregate(step - 2, inv_of[step - 2])
-            if 0 <= step - 3 < CHUNKS:
-                project(step - 3)
+            if r == 3:
+                quantise_w(1)
+            if aggregating:
+                agg_grouped = aggregate(r - 2, inv_all)
+            if turning:
+                quantise_e(r - 1, e_grouped)
+            if aggregating:
+                quantise_agg(r - 2, agg_grouped)
+            if r == 2:
+                quantise_w(0)
+            if projecting:
+                project(r - 3)
+            if starting:
+                inv_of[r] = invert(sum_of[r])

@@ -52,10 +52,10 @@ def tile_selsahead_pa_kernel(tc, q, k, feat, conv_w, conv_b, out):
         bias_rows = keep.tile([P, D], BF16)
 
         nc.vector.memset(bias_rows[:], 0.0)
-        nc.scalar.dma_start(out=bias_rows[0:1, :], in_=conv_b.rearrange("(o d) -> o d", o=1))
         nc.sync.dma_start(out=q_sb[:, 0, :], in_=q_view[:, 0, :])
         nc.sync.dma_start(out=k_sb[:, 0:2, :], in_=k_view[:, 0:2, :])
         nc.sync.dma_start(out=k_sb[:, 2:4, :], in_=k_view[:, 2:4, :])
+        nc.sync.dma_start(out=bias_rows[0:1, :], in_=conv_b.rearrange("(o d) -> o d", o=1))
         nc.sync.dma_start(out=q_sb[:, 1, :], in_=q_view[:, 1, :])
         nc.sync.dma_start(out=feat_sb[:], in_=feat_view)
         nc.sync.dma_start(out=q_sb[:, 2:4, :], in_=q_view[:, 2:4, :])
@@ -292,7 +292,6 @@ def tile_selsahead_pa_kernel(tc, q, k, feat, conv_w, conv_b, out):
             copy = scalar_copy if j % 2 == 0 else vector_copy
             fill_bank(rows_job(k_sb[:, j, :], k_t[:, :, j * P : (j + 1) * P], copy))
         fill_bank(q_job(1, scalar_copy))
-        spread_bias()
         regroup_feat()
 
         side_jobs = [
@@ -312,6 +311,8 @@ def tile_selsahead_pa_kernel(tc, q, k, feat, conv_w, conv_b, out):
             projecting = 0 <= r - 3 < CHUNKS
             if starting:
                 s_ps = scores(r, side_jobs[r])
+                if r == 0:
+                    spread_bias()
                 shift = row_shift(s_ps)
             if turning or aggregating:
                 e_grouped, inv_all = turn(e_of.get(r - 1), inv_of.get(r - 2))

@@ -24,6 +24,7 @@ HALVES = D // BANK
 PASSES = D // (P * PACK)
 BLOCKS = D // (2 * P)
 SCALE = 1.0 / 32.0
+WARM_UP = 16
 
 FLOPS = 2 * N_PROP * N_PROP * D * 2 + 2 * N_PROP * D * D
 
@@ -33,11 +34,22 @@ def tile_selsahead_pa_kernel(tc, q, k, feat, conv_w, conv_b, out):
     with ExitStack() as ctx:
         ctx.enter_context(tc.manual_schedule())
         keep = ctx.enter_context(tc.tile_pool(name="keep", bufs=1))
-        work = ctx.enter_context(tc.tile_pool(name="work", bufs=2))
-        results = ctx.enter_context(tc.tile_pool(name="results", bufs=CHUNKS))
+        work = ctx.enter_context(tc.tile_pool(name="work", bufs=CHUNKS))
+        results = ctx.enter_context(tc.tile_pool(name="results", bufs=2 * CHUNKS))
         psum_bank = ctx.enter_context(tc.psum_pool(name="psum_bank", bufs=5))
-        psum_small = ctx.enter_context(tc.psum_pool(name="psum_small", bufs=1))
+        psum_e = ctx.enter_context(tc.psum_pool(name="psum_e", bufs=1))
         psum_agg = ctx.enter_context(tc.psum_pool(name="psum_agg", bufs=2))
+
+        table_warmer = keep.tile([P, 1], F32)
+        nc.vector.memset(table_warmer[:], 0.0)
+        ones_bf16 = keep.tile([P, P], BF16)
+        nc.vector.memset(ones_bf16[:], 1.0)
+        bias_rows = keep.tile([P, D], BF16)
+        nc.vector.memset(bias_rows[:], 0.0)
+        ident_f32 = keep.tile([P, P], F32)
+        make_identity(nc, ident_f32[:])
+        ident_bf16 = keep.tile([P, P], BF16)
+        make_identity(nc, ident_bf16[:])
 
         q_view = q.rearrange("(p j) d -> p j d", j=CHUNKS)
         k_view = k.rearrange("(p j) d -> p j d", j=CHUNKS)
@@ -49,25 +61,19 @@ def tile_selsahead_pa_kernel(tc, q, k, feat, conv_w, conv_b, out):
         k_sb = keep.tile([P, CHUNKS, D], BF16)
         feat_sb = keep.tile([P, CHUNKS, D], BF16)
         w_sb = keep.tile([P, W_ROWS, D], BF16)
-        bias_rows = keep.tile([P, D], BF16)
 
-        nc.vector.memset(bias_rows[:], 0.0)
+        nc.scalar.activation(out=table_warmer[:], in_=table_warmer[:], func=ACT.Exp)
+        nc.scalar.dma_start(out=bias_rows[0:1, :], in_=conv_b.rearrange("(o d) -> o d", o=1))
         nc.sync.dma_start(out=q_sb[:, 0, :], in_=q_view[:, 0, :])
-        nc.sync.dma_start(out=k_sb[:, 0:2, :], in_=k_view[:, 0:2, :])
-        nc.sync.dma_start(out=k_sb[:, 2:4, :], in_=k_view[:, 2:4, :])
-        nc.sync.dma_start(out=bias_rows[0:1, :], in_=conv_b.rearrange("(o d) -> o d", o=1))
+        for j in range(CHUNKS):
+            nc.sync.dma_start(out=k_sb[:, j, :], in_=k_view[:, j, :])
         nc.sync.dma_start(out=q_sb[:, 1, :], in_=q_view[:, 1, :])
-        nc.sync.dma_start(out=feat_sb[:], in_=feat_view)
+        for h in range(HALVES):
+            cols = slice(h * BANK, (h + 1) * BANK)
+            nc.sync.dma_start(out=feat_sb[:, :, cols], in_=feat_view[:, :, cols])
         nc.sync.dma_start(out=q_sb[:, 2:4, :], in_=q_view[:, 2:4, :])
         for r in range(0, W_ROWS, 2):
             nc.sync.dma_start(out=w_sb[:, r : r + 2, :], in_=w_view[:, r : r + 2, :])
-
-        ident_f32 = keep.tile([P, P], F32)
-        make_identity(nc, ident_f32[:])
-        ident_bf16 = keep.tile([P, P], BF16)
-        make_identity(nc, ident_bf16[:])
-        ones_bf16 = keep.tile([P, P], BF16)
-        nc.vector.memset(ones_bf16[:], 1.0)
 
         q_t = keep.tile([P, CHUNKS, BLOCKS, P], F32)
         k_t = keep.tile([P, BLOCKS, N_PROP], F32)
@@ -84,25 +90,37 @@ def tile_selsahead_pa_kernel(tc, q, k, feat, conv_w, conv_b, out):
         agg_codes = keep.tile([P, CHUNKS, PASSES, P], U32, align_bytes=64)
         agg_scales = keep.tile([P, CHUNKS, PASSES, P], U8, align_bytes=64)
 
-        def spread_bias():
-            for h in range(HALVES):
-                cols = slice(h * BANK, (h + 1) * BANK)
-                bias_ps = psum_bank.tile([P, BANK], F32, tag="bank")
-                nc.tensor.matmul(bias_ps[:], lhsT=ones_bf16[:], rhs=bias_rows[:, cols], start=True, stop=True)
-                nc.scalar.copy(out=bias_all[:, cols], in_=bias_ps[:])
+        vector_copy = nc.vector.tensor_copy
+        scalar_copy = nc.scalar.copy
+
+        def half(h):
+            return slice(h * BANK, (h + 1) * BANK)
+
+        def bias_matmul(h):
+            bias_ps = psum_bank.tile([P, BANK], F32, tag="bank", name="bias_ps")
+            nc.tensor.matmul(bias_ps[:], lhsT=ones_bf16[:], rhs=bias_rows[:, half(h)], start=True, stop=True)
+            return bias_ps
+
+        def bias_copy(h, bias_ps):
+            nc.scalar.copy(out=bias_all[:, half(h)], in_=bias_ps[:])
 
         def add_bias_to_feat():
             for j in range(CHUNKS):
                 for h in range(HALVES):
-                    cols = slice(h * BANK, (h + 1) * BANK)
                     nc.gpsimd.tensor_tensor(
-                        out=feat_bias[:, j, cols], in0=feat_sb[:, j, cols], in1=bias_all[:, cols], op=ALU.add
+                        out=feat_bias[:, j, half(h)], in0=feat_sb[:, j, half(h)], in1=bias_all[:, half(h)], op=ALU.add
                     )
 
         def rows_job(rows, dest, copy):
             words = rows.bitcast(F32)
             sources = [words[:, c * P : (c + 1) * P] for c in range(BLOCKS)]
             return sources, lambda bank: copy(out=dest, in_=bank[:])
+
+        def q_job(j, copy):
+            return rows_job(q_sb[:, j, :], q_t[:, j, :, :], copy)
+
+        def k_job(j, copy):
+            return rows_job(k_sb[:, j, :], k_t[:, :, j * P : (j + 1) * P], copy)
 
         def w_job(pair, g, copy):
             sources = [
@@ -122,40 +140,45 @@ def tile_selsahead_pa_kernel(tc, q, k, feat, conv_w, conv_b, out):
                 nc.tensor.transpose(bank[:, slot, :], sources[slot], ident_f32[:])
             empty(bank)
 
-        def score_matmul(s_ps, j, m):
+        def new_scores():
+            return psum_bank.tile([P, N_PROP], F32, tag="bank", name="s_ps")
+
+        def score_matmul(s_ps, j, m, keys=slice(0, N_PROP)):
             c, i = divmod(m, 2)
             q_pairs = q_t[:, j, c, :].bitcast(BF16).rearrange("w (n i) -> w n i", i=2)
             k_pairs = k_t[:, c, :].bitcast(BF16).rearrange("w (n i) -> w n i", i=2)
             nc.tensor.matmul(
-                s_ps[:],
+                s_ps[:, keys],
                 lhsT=q_pairs[:, :, i],
-                rhs=k_pairs[:, :, i],
+                rhs=k_pairs[:, keys, i],
                 start=(m == 0),
                 stop=(m == 2 * BLOCKS - 1),
             )
 
-        def scores(j, jobs):
-            s_ps = psum_bank.tile([P, N_PROP], F32, tag="bank", name="s_ps")
+        def first_scores(s_ps, key_chunk):
+            for m in range(2 * BLOCKS):
+                score_matmul(s_ps, 0, m, slice(key_chunk * P, (key_chunk + 1) * P))
+
+        def scores(s_ps, j, matmuls, jobs):
             if not jobs:
-                for m in range(2 * BLOCKS):
+                for m in matmuls:
                     score_matmul(s_ps, j, m)
-                return s_ps
-            matmuls_per_job = 2 * BLOCKS // len(jobs)
+                return
+            matmuls_per_job = len(matmuls) // len(jobs)
             transposes_per_matmul = 4 // matmuls_per_job
             for number, (sources, empty) in enumerate(jobs):
                 bank = psum_bank.tile([P, 4, P], F32, tag="bank", name="t_bank")
                 for step in range(matmuls_per_job):
-                    score_matmul(s_ps, j, number * matmuls_per_job + step)
+                    score_matmul(s_ps, j, matmuls[number * matmuls_per_job + step])
                     for slot in range(step * transposes_per_matmul, (step + 1) * transposes_per_matmul):
                         nc.tensor.transpose(bank[:, slot, :], sources[slot], ident_f32[:])
                 empty(bank)
-            return s_ps
 
         def row_shift(s_ps):
             row_max = work.tile([P, 1], F32)
             nc.vector.reduce_max(out=row_max[:], in_=s_ps[:], axis=AXIS.X)
             shift = work.tile([P, 1], F32)
-            nc.vector.tensor_scalar_mul(out=shift[:], in0=row_max[:], scalar1=-SCALE)
+            nc.scalar.mul(shift[:], row_max[:], -SCALE)
             return shift
 
         def exponentials(s_ps, shift):
@@ -171,26 +194,22 @@ def tile_selsahead_pa_kernel(tc, q, k, feat, conv_w, conv_b, out):
             nc.vector.reciprocal(out=inv_sum[:], in_=row_sum[:])
             return inv_sum
 
-        def turn(e_sb, inv_sum):
-            small = psum_small.tile([P, BANK], F32)
-            e_t = small[:, 0 : BANK // 2].bitcast(BF16).rearrange("p (j n) -> p j n", j=CHUNKS)
-            inv_ps = small[:, BANK // 2 : BANK // 2 + P]
-            e_grouped = None
-            inv_all = None
-            if e_sb is not None:
-                for key_chunk in range(CHUNKS):
-                    nc.tensor.transpose(
-                        e_t[:, key_chunk, :], e_sb[:, key_chunk * P : (key_chunk + 1) * P], ident_bf16[:]
-                    )
-            if inv_sum is not None:
-                nc.tensor.transpose(inv_ps, inv_sum[:].to_broadcast([P, P]), ident_f32[:])
-            if e_sb is not None:
-                e_grouped = work.tile([P, P, PACK], BF16, align_bytes=64)
-                nc.scalar.copy(out=e_grouped[:], in_=e_t.rearrange("p j n -> p n j"))
-            if inv_sum is not None:
-                inv_all = work.tile([P, P], F32)
-                nc.scalar.copy(out=inv_all[:], in_=inv_ps)
-            return e_grouped, inv_all
+        def turn_e(e_sb):
+            e_t = psum_e.tile([P, CHUNKS, P], BF16)
+            for key_chunk in range(CHUNKS):
+                nc.tensor.transpose(
+                    e_t[:, key_chunk, :], e_sb[:, key_chunk * P : (key_chunk + 1) * P], ident_bf16[:]
+                )
+            e_grouped = work.tile([P, P, PACK], BF16, align_bytes=64)
+            nc.scalar.copy(out=e_grouped[:], in_=e_t[:].rearrange("p j n -> p n j"))
+            return e_grouped
+
+        def spread_inv(inv_sum):
+            inv_ps = psum_bank.tile([P, P], F32, tag="bank", name="inv_ps")
+            nc.tensor.transpose(inv_ps[:], inv_sum[:].to_broadcast([P, P]), ident_f32[:])
+            inv_all = work.tile([P, P], F32)
+            nc.scalar.copy(out=inv_all[:], in_=inv_ps[:])
+            return inv_all
 
         def quantise_e(j, e_grouped):
             nc.vector.quantize_mx(
@@ -199,8 +218,8 @@ def tile_selsahead_pa_kernel(tc, q, k, feat, conv_w, conv_b, out):
                 in_=e_grouped[:].rearrange("p n j -> p (n j)"),
             )
 
-        def aggregate(j, inv_all):
-            agg_grouped = work.tile([P, PASSES, P, PACK], BF16, align_bytes=64)
+        def aggregate(j):
+            banks = []
             for g in range(PASSES):
                 agg_ps = psum_agg.tile([P, PACK, P], F32)
                 for t in range(PACK):
@@ -214,9 +233,15 @@ def tile_selsahead_pa_kernel(tc, q, k, feat, conv_w, conv_b, out):
                         start=True,
                         stop=True,
                     )
+                banks.append(agg_ps)
+            return banks
+
+        def divide(banks, inv_all):
+            agg_grouped = work.tile([P, PASSES, P, PACK], BF16, align_bytes=64)
+            for g in range(PASSES):
                 nc.vector.tensor_tensor(
                     out=agg_grouped[:, g, :, :],
-                    in0=agg_ps[:].rearrange("w t n -> w n t"),
+                    in0=banks[g][:].rearrange("w t n -> w n t"),
                     in1=inv_all[:].unsqueeze(2).to_broadcast([P, P, PACK]),
                     op=ALU.mult,
                 )
@@ -229,109 +254,180 @@ def tile_selsahead_pa_kernel(tc, q, k, feat, conv_w, conv_b, out):
                 in_=agg_grouped[:].rearrange("w g n t -> w (g n t)"),
             )
 
-        def project(j):
-            result = results.tile([P, D], F32)
-            for h in range(HALVES):
-                cols = slice(h * BANK, (h + 1) * BANK)
-                out_ps = psum_bank.tile([P, BANK], F32, tag="bank", name="out_ps")
-                for g in range(PASSES):
-                    nc.tensor.matmul_mx(
-                        out=out_ps[:],
-                        lhsT=agg_codes[:, j, g, :].bitcast(FP8X4),
-                        lhsT_scale=agg_scales[:, j, g, :],
-                        rhs=w_codes[:, g, cols].bitcast(FP8X4),
-                        rhs_scale=w_scales[:, g, cols],
-                        start=(g == 0),
-                        stop=(g == PASSES - 1),
-                    )
-                nc.vector.tensor_tensor(
-                    out=result[:, cols], in0=out_ps[:], in1=feat_bias[:, j, cols], op=ALU.add
-                )
-                nc.gpsimd.tensor_scalar(
-                    out=result[:, cols], in0=result[:, cols], scalar1=math.inf, scalar2=0.0, op0=ALU.min, op1=ALU.max
-                )
-                nc.sync.dma_start(out=out_view[:, j, cols], in_=result[:, cols])
-
-        def regroup_feat():
-            sorted_src = feat_sb[:].rearrange("p j (a w i) -> p a i w j", a=BLOCKS, i=2)
-            sorted_dst = feat_grouped[:].rearrange("p (a i w) j -> p a i w j", a=BLOCKS, i=2)
-            for a in range(BLOCKS):
-                copy = nc.vector.tensor_copy if a % 2 == 0 else nc.scalar.copy
-                copy(out=sorted_dst[:, a], in_=sorted_src[:, a])
-
-        def quantise_feat():
+        def project(j, h):
+            out_ps = psum_bank.tile([P, BANK], F32, tag="bank", name="out_ps")
             for g in range(PASSES):
-                cols = slice(g * BANK, (g + 1) * BANK)
-                nc.vector.quantize_mx(
-                    out=feat_codes[:, cols].bitcast(FP8X4),
-                    scales=feat_scales[:, cols],
-                    in_=feat_grouped[:, cols, :].rearrange("p c j -> p (c j)"),
+                nc.tensor.matmul_mx(
+                    out=out_ps[:],
+                    lhsT=agg_codes[:, j, g, :].bitcast(FP8X4),
+                    lhsT_scale=agg_scales[:, j, g, :],
+                    rhs=w_codes[:, g, half(h)].bitcast(FP8X4),
+                    rhs_scale=w_scales[:, g, half(h)],
+                    start=(g == 0),
+                    stop=(g == PASSES - 1),
                 )
+            return out_ps
+
+        def relu_on_gpsimd(result):
+            nc.gpsimd.tensor_scalar(
+                out=result, in0=result, scalar1=math.inf, scalar2=0.0, op0=ALU.min, op1=ALU.max
+            )
+
+        def relu_on_scalar(result):
+            nc.scalar.activation(out=result, in_=result, func=ACT.Relu)
+
+        def residual_sum(j, h, out_ps, piece=0, pieces=1):
+            width = BANK // pieces
+            local = slice(piece * width, (piece + 1) * width)
+            cols = slice(h * BANK + piece * width, h * BANK + (piece + 1) * width)
+            result = results.tile([P, width], F32, tag="result%d" % width, name="result")
+            nc.vector.tensor_tensor(out=result[:], in0=out_ps[:, local], in1=feat_bias[:, j, cols], op=ALU.add)
+            return result
+
+        def finish(j, h, result, relu, piece=0):
+            width = result.shape[1]
+            relu(result[:])
+            cols = slice(h * BANK + piece * width, h * BANK + (piece + 1) * width)
+            nc.sync.dma_start(out=out_view[:, j, cols], in_=result[:])
+
+        def finish_on_gpsimd(j, h, out_ps):
+            result = results.tile([P, BANK], F32, tag="result%d" % BANK, name="result")
+            nc.scalar.copy(out=result[:], in_=out_ps[:])
+            nc.gpsimd.tensor_tensor(out=result[:], in0=result[:], in1=feat_bias[:, j, half(h)], op=ALU.add)
+            relu_on_gpsimd(result[:])
+            return result
+
+        def store(j, h, result):
+            nc.sync.dma_start(out=out_view[:, j, half(h)], in_=result[:])
+
+        sorted_src = feat_sb[:].rearrange("p j (a w i) -> p a i w j", a=BLOCKS, i=2)
+        sorted_dst = feat_grouped[:].rearrange("p (a i w) j -> p a i w j", a=BLOCKS, i=2)
+
+        def regroup_feat(a):
+            if a % 2 == 0:
+                nc.vector.tensor_copy(out=sorted_dst[:, a], in_=sorted_src[:, a])
+            else:
+                for i in range(2):
+                    nc.gpsimd.tensor_scalar(
+                        out=sorted_dst[:, a, i],
+                        in0=sorted_src[:, a, i],
+                        scalar1=1.0,
+                        scalar2=0.0,
+                        op0=ALU.mult,
+                        op1=ALU.add,
+                    )
+
+        def quantise_feat(g):
+            nc.vector.quantize_mx(
+                out=feat_codes[:, half(g)].bitcast(FP8X4),
+                scales=feat_scales[:, half(g)],
+                in_=feat_grouped[:, half(g), :].rearrange("p c j -> p (c j)"),
+            )
 
         def quantise_w(h):
-            cols = slice(h * BANK, (h + 1) * BANK)
             for g in range(PASSES):
                 nc.vector.quantize_mx(
-                    out=w_codes[:, g, cols].bitcast(FP8X4),
-                    scales=w_scales[:, g, cols],
-                    in_=w_grouped[:, g, cols, :].rearrange("w c u -> w (c u)").bitcast(BF16),
+                    out=w_codes[:, g, half(h)].bitcast(FP8X4),
+                    scales=w_scales[:, g, half(h)],
+                    in_=w_grouped[:, g, half(h), :].rearrange("w c u -> w (c u)").bitcast(BF16),
                 )
 
-        vector_copy = nc.vector.tensor_copy
-        scalar_copy = nc.scalar.copy
-
-        def q_job(j, copy):
-            return rows_job(q_sb[:, j, :], q_t[:, j, :, :], copy)
-
-        table_warmer = keep.tile([P, 1], F32)
-        nc.vector.memset(table_warmer[:], 0.0)
-        nc.scalar.activation(out=table_warmer[:], in_=table_warmer[:], func=ACT.Exp)
+        warm_ps = psum_bank.tile([P, P], F32, tag="bank", name="warm_ps")
+        for repeat in range(WARM_UP):
+            nc.tensor.matmul(warm_ps[:], lhsT=ones_bf16[:], rhs=ones_bf16[:], start=True, stop=True)
 
         fill_bank(q_job(0, vector_copy))
-        for j in range(CHUNKS):
-            copy = scalar_copy if j % 2 == 0 else vector_copy
-            fill_bank(rows_job(k_sb[:, j, :], k_t[:, :, j * P : (j + 1) * P], copy))
+        fill_bank(k_job(0, scalar_copy))
+        fill_bank(k_job(1, vector_copy))
+        fill_bank(k_job(2, scalar_copy))
+        fill_bank(k_job(3, vector_copy))
+        s0 = new_scores()
+        first_scores(s0, 0)
+        first_scores(s0, 1)
         fill_bank(q_job(1, scalar_copy))
-        regroup_feat()
+        first_scores(s0, 2)
+        bias0 = bias_matmul(0)
+        bias1 = bias_matmul(1)
+        first_scores(s0, 3)
+        bias_copy(0, bias0)
+        bias_copy(1, bias1)
+        regroup_feat(0)
+        regroup_feat(1)
+        shift0 = row_shift(s0)
+        e0, sum0 = exponentials(s0, shift0)
+        regroup_feat(2)
+        regroup_feat(3)
+        add_bias_to_feat()
 
-        side_jobs = [
-            [],
-            [q_job(2, vector_copy), q_job(3, scalar_copy), w_job(0, 0, vector_copy), w_job(0, 1, scalar_copy)],
-            [w_job(pair, g, vector_copy if g == 0 else scalar_copy) for pair in (1, 2) for g in range(PASSES)],
-            [w_job(3, g, scalar_copy) for g in range(PASSES)],
-        ]
+        s1 = new_scores()
+        scores(s1, 1, range(8), [q_job(2, vector_copy), q_job(3, scalar_copy)])
+        quantise_feat(0)
+        inv0 = invert(sum0)
+        shift1 = row_shift(s1)
+        e1, sum1 = exponentials(s1, shift1)
+        eg0 = turn_e(e0)
+        fill_bank(w_job(0, 0, scalar_copy))
+        inv_all0 = spread_inv(inv0)
+        fill_bank(w_job(0, 1, vector_copy))
+        quantise_feat(1)
+        quantise_e(0, eg0)
+        fill_bank(w_job(1, 0, scalar_copy))
+        fill_bank(w_job(1, 1, vector_copy))
+        eg1 = turn_e(e1)
+        agg0 = aggregate(0)
+        inv1 = invert(sum1)
+        grouped0 = divide(agg0, inv_all0)
 
-        e_of = {}
-        sum_of = {}
-        inv_of = {}
-        for r in range(CHUNKS + 3):
-            starting = r < CHUNKS
-            turning = 0 <= r - 1 < CHUNKS
-            aggregating = 0 <= r - 2 < CHUNKS
-            projecting = 0 <= r - 3 < CHUNKS
-            if starting:
-                s_ps = scores(r, side_jobs[r])
-                if r == 0:
-                    spread_bias()
-                shift = row_shift(s_ps)
-            if turning or aggregating:
-                e_grouped, inv_all = turn(e_of.get(r - 1), inv_of.get(r - 2))
-            if starting:
-                e_of[r], sum_of[r] = exponentials(s_ps, shift)
-            if r == 0:
-                quantise_feat()
-                add_bias_to_feat()
-            if r == 3:
-                quantise_w(1)
-            if aggregating:
-                agg_grouped = aggregate(r - 2, inv_all)
-            if turning:
-                quantise_e(r - 1, e_grouped)
-            if aggregating:
-                quantise_agg(r - 2, agg_grouped)
-            if r == 2:
-                quantise_w(0)
-            if projecting:
-                project(r - 3)
-            if starting:
-                inv_of[r] = invert(sum_of[r])
+        s2 = new_scores()
+        scores(s2, 2, range(0, 4), [w_job(2, 0, scalar_copy), w_job(2, 1, scalar_copy)])
+        inv_all1 = spread_inv(inv1)
+        quantise_e(1, eg1)
+        quantise_w(0)
+        quantise_agg(0, grouped0)
+        scores(s2, 2, range(4, 8), [w_job(3, 0, scalar_copy), w_job(3, 1, scalar_copy)])
+        agg1 = aggregate(1)
+        shift2 = row_shift(s2)
+        e2, sum2 = exponentials(s2, shift2)
+        grouped1 = divide(agg1, inv_all1)
+
+        s3 = new_scores()
+        scores(s3, 3, range(0, 4), [])
+        inv2 = invert(sum2)
+        eg2 = turn_e(e2)
+        quantise_agg(1, grouped1)
+        quantise_w(1)
+        quantise_e(2, eg2)
+        scores(s3, 3, range(4, 8), [])
+        inv_all2 = spread_inv(inv2)
+        out00 = project(0, 0)
+        out01 = project(0, 1)
+        shift3 = row_shift(s3)
+        e3, sum3 = exponentials(s3, shift3)
+        result01 = finish_on_gpsimd(0, 1, out01)
+        result00 = residual_sum(0, 0, out00)
+        agg2 = aggregate(2)
+        inv3 = invert(sum3)
+        grouped2 = divide(agg2, inv_all2)
+        eg3 = turn_e(e3)
+        out10 = project(1, 0)
+        out11 = project(1, 1)
+        finish(0, 0, result00, relu_on_scalar)
+        inv_all3 = spread_inv(inv3)
+        quantise_agg(2, grouped2)
+        store(0, 1, result01)
+        quantise_e(3, eg3)
+        finish(1, 0, residual_sum(1, 0, out10), relu_on_gpsimd)
+        result11 = finish_on_gpsimd(1, 1, out11)
+        agg3 = aggregate(3)
+        grouped3 = divide(agg3, inv_all3)
+        quantise_agg(3, grouped3)
+        out20 = project(2, 0)
+        out21 = project(2, 1)
+        finish(2, 0, residual_sum(2, 0, out20), relu_on_scalar)
+        out30 = project(3, 0)
+        out31 = project(3, 1)
+        finish(2, 1, residual_sum(2, 1, out21), relu_on_scalar)
+        store(1, 1, result11)
+        finish(3, 0, residual_sum(3, 0, out30), relu_on_scalar)
+        for piece in range(2):
+            finish(3, 1, residual_sum(3, 1, out31, piece, 2), relu_on_scalar, piece)

@@ -24,7 +24,6 @@ HALVES = D // BANK
 PASSES = D // (P * PACK)
 BLOCKS = D // (2 * P)
 SCALE = 1.0 / 32.0
-WARM_UP = 16
 
 FLOPS = 2 * N_PROP * N_PROP * D * 2 + 2 * N_PROP * D * D
 
@@ -48,13 +47,11 @@ def tile_selsahead_pa_kernel(tc, q, k, feat, conv_w, conv_b, out):
         nc.vector.memset(bias_rows[:], 0.0)
         ident_f32 = keep.tile([P, P], F32)
         make_identity(nc, ident_f32[:])
-        ident_bf16 = keep.tile([P, P], BF16)
-        make_identity(nc, ident_bf16[:])
 
-        q_view = q.rearrange("(p j) d -> p j d", j=CHUNKS)
-        k_view = k.rearrange("(p j) d -> p j d", j=CHUNKS)
-        feat_view = feat.rearrange("(p j) d -> p j d", j=CHUNKS)
-        out_view = out.rearrange("(p j) d -> p j d", j=CHUNKS)
+        q_view = q.rearrange("(c p i) d -> p c i d", c=2, i=2)
+        k_view = k.rearrange("(j p) d -> p j d", j=CHUNKS)
+        feat_view = feat.rearrange("(c p i) d -> p c i d", c=2, i=2)
+        out_view = out.rearrange("(c p i) d -> p c i d", c=2, i=2)
         w_view = conv_w.rearrange("(r p) d -> p r d", p=P)
 
         q_sb = keep.tile([P, CHUNKS, D], BF16)
@@ -64,14 +61,13 @@ def tile_selsahead_pa_kernel(tc, q, k, feat, conv_w, conv_b, out):
 
         nc.scalar.activation(out=table_warmer[:], in_=table_warmer[:], func=ACT.Exp)
         nc.scalar.dma_start(out=bias_rows[0:1, :], in_=conv_b.rearrange("(o d) -> o d", o=1))
-        nc.sync.dma_start(out=q_sb[:, 0, :], in_=q_view[:, 0, :])
+        nc.sync.dma_start(out=q_sb[:, 0, :], in_=q_view[:, 0, 0, :])
         for j in range(CHUNKS):
             nc.sync.dma_start(out=k_sb[:, j, :], in_=k_view[:, j, :])
-        nc.sync.dma_start(out=q_sb[:, 1, :], in_=q_view[:, 1, :])
-        for h in range(HALVES):
-            cols = slice(h * BANK, (h + 1) * BANK)
-            nc.sync.dma_start(out=feat_sb[:, :, cols], in_=feat_view[:, :, cols])
-        nc.sync.dma_start(out=q_sb[:, 2:4, :], in_=q_view[:, 2:4, :])
+        nc.sync.dma_start(out=q_sb[:, 1, :], in_=q_view[:, 0, 1, :])
+        for c in range(2):
+            nc.sync.dma_start(out=feat_sb[:, 2 * c : 2 * c + 2, :], in_=feat_view[:, c, :, :])
+        nc.sync.dma_start(out=q_sb[:, 2:4, :], in_=q_view[:, 1, :, :])
         for r in range(0, W_ROWS, 2):
             nc.sync.dma_start(out=w_sb[:, r : r + 2, :], in_=w_view[:, r : r + 2, :])
 
@@ -143,21 +139,17 @@ def tile_selsahead_pa_kernel(tc, q, k, feat, conv_w, conv_b, out):
         def new_scores():
             return psum_bank.tile([P, N_PROP], F32, tag="bank", name="s_ps")
 
-        def score_matmul(s_ps, j, m, keys=slice(0, N_PROP)):
+        def score_matmul(s_ps, j, m):
             c, i = divmod(m, 2)
             q_pairs = q_t[:, j, c, :].bitcast(BF16).rearrange("w (n i) -> w n i", i=2)
             k_pairs = k_t[:, c, :].bitcast(BF16).rearrange("w (n i) -> w n i", i=2)
             nc.tensor.matmul(
-                s_ps[:, keys],
+                s_ps[:],
                 lhsT=q_pairs[:, :, i],
-                rhs=k_pairs[:, keys, i],
+                rhs=k_pairs[:, :, i],
                 start=(m == 0),
                 stop=(m == 2 * BLOCKS - 1),
             )
-
-        def first_scores(s_ps, key_chunk):
-            for m in range(2 * BLOCKS):
-                score_matmul(s_ps, 0, m, slice(key_chunk * P, (key_chunk + 1) * P))
 
         def scores(s_ps, j, matmuls, jobs):
             if not jobs:
@@ -195,13 +187,12 @@ def tile_selsahead_pa_kernel(tc, q, k, feat, conv_w, conv_b, out):
             return inv_sum
 
         def turn_e(e_sb):
-            e_t = psum_e.tile([P, CHUNKS, P], BF16)
-            for key_chunk in range(CHUNKS):
-                nc.tensor.transpose(
-                    e_t[:, key_chunk, :], e_sb[:, key_chunk * P : (key_chunk + 1) * P], ident_bf16[:]
-                )
-            e_grouped = work.tile([P, P, PACK], BF16, align_bytes=64)
-            nc.scalar.copy(out=e_grouped[:], in_=e_t[:].rearrange("p j n -> p n j"))
+            words = e_sb[:].bitcast(F32)
+            e_t = psum_e.tile([P, 2, P], F32)
+            for c in range(2):
+                nc.tensor.transpose(e_t[:, c, :], words[:, c * P : (c + 1) * P], ident_f32[:])
+            e_grouped = work.tile([P, P, 2], F32, align_bytes=64)
+            nc.scalar.copy(out=e_grouped[:], in_=e_t[:].rearrange("p c n -> p n c"))
             return e_grouped
 
         def spread_inv(inv_sum):
@@ -215,7 +206,7 @@ def tile_selsahead_pa_kernel(tc, q, k, feat, conv_w, conv_b, out):
             nc.vector.quantize_mx(
                 out=e_codes[:, j, :].bitcast(FP8X4),
                 scales=e_scales[:, j, :],
-                in_=e_grouped[:].rearrange("p n j -> p (n j)"),
+                in_=e_grouped[:].rearrange("p n c -> p (n c)").bitcast(BF16),
             )
 
         def aggregate(j):
@@ -288,34 +279,14 @@ def tile_selsahead_pa_kernel(tc, q, k, feat, conv_w, conv_b, out):
             width = result.shape[1]
             relu(result[:])
             cols = slice(h * BANK + piece * width, h * BANK + (piece + 1) * width)
-            nc.sync.dma_start(out=out_view[:, j, cols], in_=result[:])
-
-        def finish_on_gpsimd(j, h, out_ps):
-            result = results.tile([P, BANK], F32, tag="result%d" % BANK, name="result")
-            nc.scalar.copy(out=result[:], in_=out_ps[:])
-            nc.gpsimd.tensor_tensor(out=result[:], in0=result[:], in1=feat_bias[:, j, half(h)], op=ALU.add)
-            relu_on_gpsimd(result[:])
-            return result
-
-        def store(j, h, result):
-            nc.sync.dma_start(out=out_view[:, j, half(h)], in_=result[:])
+            nc.sync.dma_start(out=out_view[:, j // 2, j % 2, cols], in_=result[:])
 
         sorted_src = feat_sb[:].rearrange("p j (a w i) -> p a i w j", a=BLOCKS, i=2)
         sorted_dst = feat_grouped[:].rearrange("p (a i w) j -> p a i w j", a=BLOCKS, i=2)
 
         def regroup_feat(a):
-            if a % 2 == 0:
-                nc.vector.tensor_copy(out=sorted_dst[:, a], in_=sorted_src[:, a])
-            else:
-                for i in range(2):
-                    nc.gpsimd.tensor_scalar(
-                        out=sorted_dst[:, a, i],
-                        in0=sorted_src[:, a, i],
-                        scalar1=1.0,
-                        scalar2=0.0,
-                        op0=ALU.mult,
-                        op1=ALU.add,
-                    )
+            copy = scalar_copy if a == BLOCKS - 1 else vector_copy
+            copy(out=sorted_dst[:, a], in_=sorted_src[:, a])
 
         def quantise_feat(g):
             nc.vector.quantize_mx(
@@ -332,23 +303,16 @@ def tile_selsahead_pa_kernel(tc, q, k, feat, conv_w, conv_b, out):
                     in_=w_grouped[:, g, half(h), :].rearrange("w c u -> w (c u)").bitcast(BF16),
                 )
 
-        warm_ps = psum_bank.tile([P, P], F32, tag="bank", name="warm_ps")
-        for repeat in range(WARM_UP):
-            nc.tensor.matmul(warm_ps[:], lhsT=ones_bf16[:], rhs=ones_bf16[:], start=True, stop=True)
-
         fill_bank(q_job(0, vector_copy))
         fill_bank(k_job(0, scalar_copy))
         fill_bank(k_job(1, vector_copy))
         fill_bank(k_job(2, scalar_copy))
         fill_bank(k_job(3, vector_copy))
         s0 = new_scores()
-        first_scores(s0, 0)
-        first_scores(s0, 1)
         fill_bank(q_job(1, scalar_copy))
-        first_scores(s0, 2)
+        scores(s0, 0, range(8), [])
         bias0 = bias_matmul(0)
         bias1 = bias_matmul(1)
-        first_scores(s0, 3)
         bias_copy(0, bias0)
         bias_copy(1, bias1)
         regroup_feat(0)
@@ -403,8 +367,8 @@ def tile_selsahead_pa_kernel(tc, q, k, feat, conv_w, conv_b, out):
         out01 = project(0, 1)
         shift3 = row_shift(s3)
         e3, sum3 = exponentials(s3, shift3)
-        result01 = finish_on_gpsimd(0, 1, out01)
         result00 = residual_sum(0, 0, out00)
+        result01 = residual_sum(0, 1, out01)
         agg2 = aggregate(2)
         inv3 = invert(sum3)
         grouped2 = divide(agg2, inv_all2)
@@ -414,10 +378,11 @@ def tile_selsahead_pa_kernel(tc, q, k, feat, conv_w, conv_b, out):
         finish(0, 0, result00, relu_on_scalar)
         inv_all3 = spread_inv(inv3)
         quantise_agg(2, grouped2)
-        store(0, 1, result01)
+        finish(0, 1, result01, relu_on_gpsimd)
         quantise_e(3, eg3)
         finish(1, 0, residual_sum(1, 0, out10), relu_on_gpsimd)
-        result11 = finish_on_gpsimd(1, 1, out11)
+        result11 = residual_sum(1, 1, out11)
+        finish(1, 1, result11, relu_on_gpsimd)
         agg3 = aggregate(3)
         grouped3 = divide(agg3, inv_all3)
         quantise_agg(3, grouped3)
@@ -427,7 +392,6 @@ def tile_selsahead_pa_kernel(tc, q, k, feat, conv_w, conv_b, out):
         out30 = project(3, 0)
         out31 = project(3, 1)
         finish(2, 1, residual_sum(2, 1, out21), relu_on_scalar)
-        store(1, 1, result11)
         finish(3, 0, residual_sum(3, 0, out30), relu_on_scalar)
         for piece in range(2):
             finish(3, 1, residual_sum(3, 1, out31, piece, 2), relu_on_scalar, piece)

@@ -41,6 +41,8 @@ def tile_selsahead_pa_kernel(tc, q, k, feat, conv_w, conv_b, out):
 
         table_warmer = keep.tile([P, 1], F32)
         nc.vector.memset(table_warmer[:], 0.0)
+        ones_f32 = keep.tile([P, P], F32)
+        nc.vector.memset(ones_f32[:], 1.0)
         ones_bf16 = keep.tile([P, P], BF16)
         nc.vector.memset(ones_bf16[:], 1.0)
         bias_rows = keep.tile([P, D], BF16)
@@ -60,10 +62,10 @@ def tile_selsahead_pa_kernel(tc, q, k, feat, conv_w, conv_b, out):
         w_sb = keep.tile([P, W_ROWS, D], BF16)
 
         nc.scalar.activation(out=table_warmer[:], in_=table_warmer[:], func=ACT.Exp)
-        nc.scalar.dma_start(out=bias_rows[0:1, :], in_=conv_b.rearrange("(o d) -> o d", o=1))
         nc.sync.dma_start(out=q_sb[:, 0, :], in_=q_view[:, 0, 0, :])
         for j in range(CHUNKS):
             nc.sync.dma_start(out=k_sb[:, j, :], in_=k_view[:, j, :])
+        nc.sync.dma_start(out=bias_rows[0:1, :], in_=conv_b.rearrange("(o d) -> o d", o=1))
         nc.sync.dma_start(out=q_sb[:, 1, :], in_=q_view[:, 0, 1, :])
         for c in range(2):
             nc.sync.dma_start(out=feat_sb[:, 2 * c : 2 * c + 2, :], in_=feat_view[:, c, :, :])
@@ -227,16 +229,16 @@ def tile_selsahead_pa_kernel(tc, q, k, feat, conv_w, conv_b, out):
                 banks.append(agg_ps)
             return banks
 
-        def divide(banks, inv_all):
-            agg_grouped = work.tile([P, PASSES, P, PACK], BF16, align_bytes=64)
-            for g in range(PASSES):
-                nc.vector.tensor_tensor(
-                    out=agg_grouped[:, g, :, :],
-                    in0=banks[g][:].rearrange("w t n -> w n t"),
-                    in1=inv_all[:].unsqueeze(2).to_broadcast([P, P, PACK]),
-                    op=ALU.mult,
-                )
-            return agg_grouped
+        def new_grouped():
+            return work.tile([P, PASSES, P, PACK], BF16, align_bytes=64, name="agg_grouped")
+
+        def divide(g, agg_ps, inv_all, agg_grouped):
+            nc.vector.tensor_tensor(
+                out=agg_grouped[:, g, :, :],
+                in0=agg_ps[:].rearrange("w t n -> w n t"),
+                in1=inv_all[:].unsqueeze(2).to_broadcast([P, P, PACK]),
+                op=ALU.mult,
+            )
 
         def quantise_agg(j, agg_grouped):
             nc.vector.quantize_mx(
@@ -295,103 +297,117 @@ def tile_selsahead_pa_kernel(tc, q, k, feat, conv_w, conv_b, out):
                 in_=feat_grouped[:, half(g), :].rearrange("p c j -> p (c j)"),
             )
 
-        def quantise_w(h):
-            for g in range(PASSES):
-                nc.vector.quantize_mx(
-                    out=w_codes[:, g, half(h)].bitcast(FP8X4),
-                    scales=w_scales[:, g, half(h)],
-                    in_=w_grouped[:, g, half(h), :].rearrange("w c u -> w (c u)").bitcast(BF16),
-                )
+        def quantise_w(h, g):
+            nc.vector.quantize_mx(
+                out=w_codes[:, g, half(h)].bitcast(FP8X4),
+                scales=w_scales[:, g, half(h)],
+                in_=w_grouped[:, g, half(h), :].rearrange("w c u -> w (c u)").bitcast(BF16),
+            )
 
+        warm_ps = psum_e.tile([P, 2, P], F32, name="e_t")
+
+        def warm(repeats):
+            for repeat in range(repeats):
+                nc.tensor.matmul(warm_ps[:, 0, :], lhsT=ones_f32[:], rhs=ones_f32[:], start=True, stop=True)
+
+        warm(4)
         fill_bank(q_job(0, vector_copy))
-        fill_bank(k_job(0, scalar_copy))
-        fill_bank(k_job(1, vector_copy))
-        fill_bank(k_job(2, scalar_copy))
-        fill_bank(k_job(3, vector_copy))
-        s0 = new_scores()
+        for j in range(CHUNKS):
+            fill_bank(k_job(j, scalar_copy if j % 2 == 0 else vector_copy))
+            warm(1)
         fill_bank(q_job(1, scalar_copy))
-        scores(s0, 0, range(8), [])
         bias0 = bias_matmul(0)
         bias1 = bias_matmul(1)
         bias_copy(0, bias0)
         bias_copy(1, bias1)
+        s0 = new_scores()
+        scores(s0, 0, range(8), [])
         regroup_feat(0)
-        regroup_feat(1)
         shift0 = row_shift(s0)
         e0, sum0 = exponentials(s0, shift0)
-        regroup_feat(2)
-        regroup_feat(3)
+        for a in range(1, BLOCKS):
+            regroup_feat(a)
         add_bias_to_feat()
 
         s1 = new_scores()
         scores(s1, 1, range(8), [q_job(2, vector_copy), q_job(3, scalar_copy)])
-        quantise_feat(0)
         inv0 = invert(sum0)
+        quantise_feat(0)
         shift1 = row_shift(s1)
         e1, sum1 = exponentials(s1, shift1)
-        eg0 = turn_e(e0)
-        fill_bank(w_job(0, 0, scalar_copy))
-        inv_all0 = spread_inv(inv0)
-        fill_bank(w_job(0, 1, vector_copy))
-        quantise_feat(1)
-        quantise_e(0, eg0)
-        fill_bank(w_job(1, 0, scalar_copy))
-        fill_bank(w_job(1, 1, vector_copy))
-        eg1 = turn_e(e1)
-        agg0 = aggregate(0)
-        inv1 = invert(sum1)
-        grouped0 = divide(agg0, inv_all0)
 
         s2 = new_scores()
-        scores(s2, 2, range(0, 4), [w_job(2, 0, scalar_copy), w_job(2, 1, scalar_copy)])
+        scores(s2, 2, range(0, 4), [])
+        eg0 = turn_e(e0)
+        fill_bank(w_job(0, 0, scalar_copy))
+        fill_bank(w_job(0, 1, scalar_copy))
+        inv_all0 = spread_inv(inv0)
+        quantise_feat(1)
+        quantise_e(0, eg0)
+        inv1 = invert(sum1)
+        scores(s2, 2, range(4, 8), [w_job(1, 0, vector_copy)])
+        eg1 = turn_e(e1)
+        fill_bank(w_job(1, 1, scalar_copy))
+        s3 = new_scores()
+        scores(s3, 3, range(0, 2), [])
         inv_all1 = spread_inv(inv1)
+        agg0 = aggregate(0)
         quantise_e(1, eg1)
-        quantise_w(0)
-        quantise_agg(0, grouped0)
-        scores(s2, 2, range(4, 8), [w_job(3, 0, scalar_copy), w_job(3, 1, scalar_copy)])
-        agg1 = aggregate(1)
         shift2 = row_shift(s2)
         e2, sum2 = exponentials(s2, shift2)
-        grouped1 = divide(agg1, inv_all1)
-
-        s3 = new_scores()
-        scores(s3, 3, range(0, 4), [])
+        grouped0 = new_grouped()
+        divide(0, agg0[0], inv_all0, grouped0)
+        divide(1, agg0[1], inv_all0, grouped0)
+        quantise_w(0, 0)
+        quantise_w(0, 1)
+        quantise_agg(0, grouped0)
+        fill_bank(w_job(2, 0, scalar_copy))
+        fill_bank(w_job(3, 0, scalar_copy))
         inv2 = invert(sum2)
+        scores(s3, 3, range(2, 4), [w_job(2, 1, scalar_copy)])
         eg2 = turn_e(e2)
-        quantise_agg(1, grouped1)
-        quantise_w(1)
+        agg1 = aggregate(1)
+        grouped1 = new_grouped()
+        divide(0, agg1[0], inv_all1, grouped1)
+        quantise_w(1, 0)
         quantise_e(2, eg2)
-        scores(s3, 3, range(4, 8), [])
+        divide(1, agg1[1], inv_all1, grouped1)
+        scores(s3, 3, range(4, 8), [w_job(3, 1, scalar_copy)])
         inv_all2 = spread_inv(inv2)
-        out00 = project(0, 0)
-        out01 = project(0, 1)
         shift3 = row_shift(s3)
         e3, sum3 = exponentials(s3, shift3)
-        result00 = residual_sum(0, 0, out00)
-        result01 = residual_sum(0, 1, out01)
+        quantise_agg(1, grouped1)
+        out00 = project(0, 0)
         agg2 = aggregate(2)
+        result00 = residual_sum(0, 0, out00)
+        quantise_w(1, 1)
         inv3 = invert(sum3)
-        grouped2 = divide(agg2, inv_all2)
-        eg3 = turn_e(e3)
         out10 = project(1, 0)
-        out11 = project(1, 1)
+        eg3 = turn_e(e3)
         finish(0, 0, result00, relu_on_scalar)
+        out01 = project(0, 1)
         inv_all3 = spread_inv(inv3)
-        quantise_agg(2, grouped2)
-        finish(0, 1, result01, relu_on_gpsimd)
+        grouped2 = new_grouped()
+        divide(0, agg2[0], inv_all2, grouped2)
+        divide(1, agg2[1], inv_all2, grouped2)
         quantise_e(3, eg3)
-        finish(1, 0, residual_sum(1, 0, out10), relu_on_gpsimd)
-        result11 = residual_sum(1, 1, out11)
-        finish(1, 1, result11, relu_on_gpsimd)
+        finish(0, 1, residual_sum(0, 1, out01), relu_on_gpsimd)
         agg3 = aggregate(3)
-        grouped3 = divide(agg3, inv_all3)
-        quantise_agg(3, grouped3)
+        quantise_agg(2, grouped2)
+        finish(1, 0, residual_sum(1, 0, out10), relu_on_scalar)
+        out11 = project(1, 1)
+        grouped3 = new_grouped()
+        divide(0, agg3[0], inv_all3, grouped3)
+        divide(1, agg3[1], inv_all3, grouped3)
         out20 = project(2, 0)
+        finish(1, 1, residual_sum(1, 1, out11), relu_on_gpsimd)
+        quantise_agg(3, grouped3)
         out21 = project(2, 1)
         finish(2, 0, residual_sum(2, 0, out20), relu_on_scalar)
         out30 = project(3, 0)
+        result21 = residual_sum(2, 1, out21)
         out31 = project(3, 1)
-        finish(2, 1, residual_sum(2, 1, out21), relu_on_scalar)
         finish(3, 0, residual_sum(3, 0, out30), relu_on_scalar)
+        finish(2, 1, result21, relu_on_gpsimd)
         for piece in range(2):
             finish(3, 1, residual_sum(3, 1, out31, piece, 2), relu_on_scalar, piece)

@@ -102,12 +102,10 @@ def tile_selsahead_pa_kernel(tc, q, k, feat, conv_w, conv_b, out):
         def bias_copy(h, bias_ps):
             nc.scalar.copy(out=bias_all[:, half(h)], in_=bias_ps[:])
 
-        def add_bias_to_feat():
-            for j in range(CHUNKS):
-                for h in range(HALVES):
-                    nc.gpsimd.tensor_tensor(
-                        out=feat_bias[:, j, half(h)], in0=feat_sb[:, j, half(h)], in1=bias_all[:, half(h)], op=ALU.add
-                    )
+        def add_bias_to_feat(j, h):
+            nc.gpsimd.tensor_tensor(
+                out=feat_bias[:, j, half(h)], in0=feat_sb[:, j, half(h)], in1=bias_all[:, half(h)], op=ALU.add
+            )
 
         def rows_job(rows, dest, copy):
             words = rows.bitcast(F32)
@@ -141,38 +139,31 @@ def tile_selsahead_pa_kernel(tc, q, k, feat, conv_w, conv_b, out):
         def new_scores():
             return psum_bank.tile([P, N_PROP], F32, tag="bank", name="s_ps")
 
-        def score_matmul(s_ps, j, m):
+        def score_matmul(s_ps, j, m, keys=slice(0, N_PROP)):
             c, i = divmod(m, 2)
             q_pairs = q_t[:, j, c, :].bitcast(BF16).rearrange("w (n i) -> w n i", i=2)
             k_pairs = k_t[:, c, :].bitcast(BF16).rearrange("w (n i) -> w n i", i=2)
             nc.tensor.matmul(
-                s_ps[:],
+                s_ps[:, keys],
                 lhsT=q_pairs[:, :, i],
-                rhs=k_pairs[:, :, i],
+                rhs=k_pairs[:, keys, i],
                 start=(m == 0),
                 stop=(m == 2 * BLOCKS - 1),
             )
 
-        def scores(s_ps, j, matmuls, jobs):
-            if not jobs:
-                for m in matmuls:
-                    score_matmul(s_ps, j, m)
-                return
-            matmuls_per_job = len(matmuls) // len(jobs)
-            transposes_per_matmul = 4 // matmuls_per_job
-            for number, (sources, empty) in enumerate(jobs):
-                bank = psum_bank.tile([P, 4, P], F32, tag="bank", name="t_bank")
-                for step in range(matmuls_per_job):
-                    score_matmul(s_ps, j, matmuls[number * matmuls_per_job + step])
-                    for slot in range(step * transposes_per_matmul, (step + 1) * transposes_per_matmul):
-                        nc.tensor.transpose(bank[:, slot, :], sources[slot], ident_f32[:])
-                empty(bank)
+        def first_scores(s_ps, half_of_keys):
+            for m in range(2 * BLOCKS):
+                score_matmul(s_ps, 0, m, slice(half_of_keys * 2 * P, (half_of_keys + 1) * 2 * P))
+
+        def scores(s_ps, j, matmuls):
+            for m in matmuls:
+                score_matmul(s_ps, j, m)
 
         def row_shift(s_ps):
             row_max = work.tile([P, 1], F32)
             nc.vector.reduce_max(out=row_max[:], in_=s_ps[:], axis=AXIS.X)
             shift = work.tile([P, 1], F32)
-            nc.scalar.mul(shift[:], row_max[:], -SCALE)
+            nc.vector.tensor_scalar_mul(out=shift[:], in0=row_max[:], scalar1=-SCALE)
             return shift
 
         def exponentials(s_ps, shift):
@@ -229,16 +220,16 @@ def tile_selsahead_pa_kernel(tc, q, k, feat, conv_w, conv_b, out):
                 banks.append(agg_ps)
             return banks
 
-        def new_grouped():
-            return work.tile([P, PASSES, P, PACK], BF16, align_bytes=64, name="agg_grouped")
-
-        def divide(g, agg_ps, inv_all, agg_grouped):
-            nc.vector.tensor_tensor(
-                out=agg_grouped[:, g, :, :],
-                in0=agg_ps[:].rearrange("w t n -> w n t"),
-                in1=inv_all[:].unsqueeze(2).to_broadcast([P, P, PACK]),
-                op=ALU.mult,
-            )
+        def divide(banks, inv_all):
+            agg_grouped = work.tile([P, PASSES, P, PACK], BF16, align_bytes=64)
+            for g in range(PASSES):
+                nc.vector.tensor_tensor(
+                    out=agg_grouped[:, g, :, :],
+                    in0=banks[g][:].rearrange("w t n -> w n t"),
+                    in1=inv_all[:].unsqueeze(2).to_broadcast([P, P, PACK]),
+                    op=ALU.mult,
+                )
+            return agg_grouped
 
         def quantise_agg(j, agg_grouped):
             nc.vector.quantize_mx(
@@ -287,8 +278,7 @@ def tile_selsahead_pa_kernel(tc, q, k, feat, conv_w, conv_b, out):
         sorted_dst = feat_grouped[:].rearrange("p (a i w) j -> p a i w j", a=BLOCKS, i=2)
 
         def regroup_feat(a):
-            copy = scalar_copy if a == BLOCKS - 1 else vector_copy
-            copy(out=sorted_dst[:, a], in_=sorted_src[:, a])
+            nc.scalar.copy(out=sorted_dst[:, a], in_=sorted_src[:, a])
 
         def quantise_feat(g):
             nc.vector.quantize_mx(
@@ -311,103 +301,107 @@ def tile_selsahead_pa_kernel(tc, q, k, feat, conv_w, conv_b, out):
                 nc.tensor.matmul(warm_ps[:, 0, :], lhsT=ones_f32[:], rhs=ones_f32[:], start=True, stop=True)
 
         warm(4)
-        fill_bank(q_job(0, vector_copy))
-        for j in range(CHUNKS):
-            fill_bank(k_job(j, scalar_copy if j % 2 == 0 else vector_copy))
-            warm(1)
-        fill_bank(q_job(1, scalar_copy))
+        fill_bank(q_job(0, scalar_copy))
+        fill_bank(k_job(0, vector_copy))
+        warm(1)
+        fill_bank(k_job(1, vector_copy))
+        warm(1)
+        fill_bank(k_job(2, scalar_copy))
+        fill_bank(k_job(3, vector_copy))
+        fill_bank(q_job(1, vector_copy))
         bias0 = bias_matmul(0)
         bias1 = bias_matmul(1)
         bias_copy(0, bias0)
         bias_copy(1, bias1)
         s0 = new_scores()
-        scores(s0, 0, range(8), [])
+        first_scores(s0, 0)
+        first_scores(s0, 1)
         regroup_feat(0)
+        halves = [(j, h) for j in range(CHUNKS) for h in range(HALVES)]
+        for j, h in halves[:-1]:
+            add_bias_to_feat(j, h)
+        regroup_feat(1)
         shift0 = row_shift(s0)
         e0, sum0 = exponentials(s0, shift0)
-        for a in range(1, BLOCKS):
-            regroup_feat(a)
-        add_bias_to_feat()
 
         s1 = new_scores()
-        scores(s1, 1, range(8), [q_job(2, vector_copy), q_job(3, scalar_copy)])
+        scores(s1, 1, range(0, 4))
+        fill_bank(q_job(2, vector_copy))
+        scores(s1, 1, range(4, 8))
+        regroup_feat(2)
+        fill_bank(q_job(3, scalar_copy))
         inv0 = invert(sum0)
-        quantise_feat(0)
         shift1 = row_shift(s1)
+        fill_bank(w_job(0, 0, vector_copy))
         e1, sum1 = exponentials(s1, shift1)
 
         s2 = new_scores()
-        scores(s2, 2, range(0, 4), [])
+        scores(s2, 2, range(0, 4))
+        quantise_feat(0)
         eg0 = turn_e(e0)
-        fill_bank(w_job(0, 0, scalar_copy))
-        fill_bank(w_job(0, 1, scalar_copy))
         inv_all0 = spread_inv(inv0)
+        regroup_feat(3)
+        scores(s2, 2, range(4, 8))
+        shift2 = row_shift(s2)
+        inv1 = invert(sum1)
+        e2, sum2 = exponentials(s2, shift2)
+
+        s3 = new_scores()
+        scores(s3, 3, range(0, 4))
         quantise_feat(1)
         quantise_e(0, eg0)
-        inv1 = invert(sum1)
-        scores(s2, 2, range(4, 8), [w_job(1, 0, vector_copy)])
         eg1 = turn_e(e1)
-        fill_bank(w_job(1, 1, scalar_copy))
-        s3 = new_scores()
-        scores(s3, 3, range(0, 2), [])
-        inv_all1 = spread_inv(inv1)
-        agg0 = aggregate(0)
+        fill_bank(w_job(1, 0, scalar_copy))
+        scores(s3, 3, range(4, 8))
+        fill_bank(w_job(0, 1, scalar_copy))
+        inv2 = invert(sum2)
         quantise_e(1, eg1)
-        shift2 = row_shift(s2)
-        e2, sum2 = exponentials(s2, shift2)
-        grouped0 = new_grouped()
-        divide(0, agg0[0], inv_all0, grouped0)
-        divide(1, agg0[1], inv_all0, grouped0)
+        shift3 = row_shift(s3)
+        agg0 = aggregate(0)
+        e3, sum3 = exponentials(s3, shift3)
+        eg2 = turn_e(e2)
+        inv_all1 = spread_inv(inv1)
+        fill_bank(w_job(1, 1, scalar_copy))
+        grouped0 = divide(agg0, inv_all0)
         quantise_w(0, 0)
-        quantise_w(0, 1)
         quantise_agg(0, grouped0)
+        quantise_w(0, 1)
+        inv3 = invert(sum3)
+        agg1 = aggregate(1)
+        quantise_e(2, eg2)
+        eg3 = turn_e(e3)
+        inv_all2 = spread_inv(inv2)
         fill_bank(w_job(2, 0, scalar_copy))
         fill_bank(w_job(3, 0, scalar_copy))
-        inv2 = invert(sum2)
-        scores(s3, 3, range(2, 4), [w_job(2, 1, scalar_copy)])
-        eg2 = turn_e(e2)
-        agg1 = aggregate(1)
-        grouped1 = new_grouped()
-        divide(0, agg1[0], inv_all1, grouped1)
-        quantise_w(1, 0)
-        quantise_e(2, eg2)
-        divide(1, agg1[1], inv_all1, grouped1)
-        scores(s3, 3, range(4, 8), [w_job(3, 1, scalar_copy)])
-        inv_all2 = spread_inv(inv2)
-        shift3 = row_shift(s3)
-        e3, sum3 = exponentials(s3, shift3)
-        quantise_agg(1, grouped1)
-        out00 = project(0, 0)
-        agg2 = aggregate(2)
-        result00 = residual_sum(0, 0, out00)
-        quantise_w(1, 1)
-        inv3 = invert(sum3)
-        out10 = project(1, 0)
-        eg3 = turn_e(e3)
-        finish(0, 0, result00, relu_on_scalar)
-        out01 = project(0, 1)
-        inv_all3 = spread_inv(inv3)
-        grouped2 = new_grouped()
-        divide(0, agg2[0], inv_all2, grouped2)
-        divide(1, agg2[1], inv_all2, grouped2)
+        grouped1 = divide(agg1, inv_all1)
         quantise_e(3, eg3)
-        finish(0, 1, residual_sum(0, 1, out01), relu_on_gpsimd)
-        agg3 = aggregate(3)
+        quantise_agg(1, grouped1)
+        inv_all3 = spread_inv(inv3)
+        agg2 = aggregate(2)
+        out00 = project(0, 0)
+        grouped2 = divide(agg2, inv_all2)
+        quantise_w(1, 0)
+        finish(0, 0, residual_sum(0, 0, out00), relu_on_gpsimd)
         quantise_agg(2, grouped2)
-        finish(1, 0, residual_sum(1, 0, out10), relu_on_scalar)
-        out11 = project(1, 1)
-        grouped3 = new_grouped()
-        divide(0, agg3[0], inv_all3, grouped3)
-        divide(1, agg3[1], inv_all3, grouped3)
+        fill_bank(w_job(2, 1, scalar_copy))
+        fill_bank(w_job(3, 1, scalar_copy))
+        agg3 = aggregate(3)
+        out10 = project(1, 0)
+        grouped3 = divide(agg3, inv_all3)
         out20 = project(2, 0)
-        finish(1, 1, residual_sum(1, 1, out11), relu_on_gpsimd)
+        finish(1, 0, residual_sum(1, 0, out10), relu_on_gpsimd)
         quantise_agg(3, grouped3)
-        out21 = project(2, 1)
+        quantise_w(1, 1)
+        add_bias_to_feat(*halves[-1])
         finish(2, 0, residual_sum(2, 0, out20), relu_on_scalar)
         out30 = project(3, 0)
-        result21 = residual_sum(2, 1, out21)
-        out31 = project(3, 1)
+        out01 = project(0, 1)
+        out11 = project(1, 1)
         finish(3, 0, residual_sum(3, 0, out30), relu_on_scalar)
-        finish(2, 1, result21, relu_on_gpsimd)
+        out21 = project(2, 1)
+        finish(0, 1, residual_sum(0, 1, out01), relu_on_scalar)
+        out31 = project(3, 1)
+        finish(1, 1, residual_sum(1, 1, out11), relu_on_scalar)
+        finish(2, 1, residual_sum(2, 1, out21), relu_on_scalar)
         for piece in range(2):
             finish(3, 1, residual_sum(3, 1, out31, piece, 2), relu_on_scalar, piece)

@@ -11,7 +11,6 @@ U8 = mybir.dt.uint8
 FP8X4 = mybir.dt.float8_e4m3fn_x4
 ALU = mybir.AluOpType
 ACT = mybir.ActivationFunctionType
-AXIS = mybir.AxisListType
 
 P = 128
 PACK = 4
@@ -160,10 +159,17 @@ def tile_selsahead_pa_kernel(tc, q, k, feat, conv_w, conv_b, out):
                 score_matmul(s_ps, j, m)
 
         def row_shift(s_ps):
-            row_max = work.tile([P, 1], F32)
-            nc.vector.reduce_max(out=row_max[:], in_=s_ps[:], axis=AXIS.X)
+            scaled = work.tile([P, N_PROP], BF16)
             shift = work.tile([P, 1], F32)
-            nc.vector.tensor_scalar_mul(out=shift[:], in0=row_max[:], scalar1=-SCALE)
+            nc.vector.tensor_scalar(
+                out=scaled[:],
+                in0=s_ps[:],
+                scalar1=-SCALE,
+                scalar2=None,
+                op0=ALU.mult,
+                op1=ALU.min,
+                accum_out=shift[:],
+            )
             return shift
 
         def exponentials(s_ps, shift):
@@ -220,16 +226,16 @@ def tile_selsahead_pa_kernel(tc, q, k, feat, conv_w, conv_b, out):
                 banks.append(agg_ps)
             return banks
 
-        def divide(banks, inv_all):
-            agg_grouped = work.tile([P, PASSES, P, PACK], BF16, align_bytes=64)
-            for g in range(PASSES):
-                nc.vector.tensor_tensor(
-                    out=agg_grouped[:, g, :, :],
-                    in0=banks[g][:].rearrange("w t n -> w n t"),
-                    in1=inv_all[:].unsqueeze(2).to_broadcast([P, P, PACK]),
-                    op=ALU.mult,
-                )
-            return agg_grouped
+        def new_grouped():
+            return work.tile([P, PASSES, P, PACK], BF16, align_bytes=64, name="agg_grouped")
+
+        def divide(g, banks, inv_all, agg_grouped):
+            nc.vector.tensor_tensor(
+                out=agg_grouped[:, g, :, :],
+                in0=banks[g][:].rearrange("w t n -> w n t"),
+                in1=inv_all[:].unsqueeze(2).to_broadcast([P, P, PACK]),
+                op=ALU.mult,
+            )
 
         def quantise_agg(j, agg_grouped):
             nc.vector.quantize_mx(
@@ -257,6 +263,9 @@ def tile_selsahead_pa_kernel(tc, q, k, feat, conv_w, conv_b, out):
                 out=result, in0=result, scalar1=math.inf, scalar2=0.0, op0=ALU.min, op1=ALU.max
             )
 
+        def relu_on_vector(result):
+            nc.vector.tensor_scalar_max(out=result, in0=result, scalar1=0.0)
+
         def relu_on_scalar(result):
             nc.scalar.activation(out=result, in_=result, func=ACT.Relu)
 
@@ -278,7 +287,8 @@ def tile_selsahead_pa_kernel(tc, q, k, feat, conv_w, conv_b, out):
         sorted_dst = feat_grouped[:].rearrange("p (a i w) j -> p a i w j", a=BLOCKS, i=2)
 
         def regroup_feat(a):
-            nc.scalar.copy(out=sorted_dst[:, a], in_=sorted_src[:, a])
+            copy = vector_copy if a == 0 else scalar_copy
+            copy(out=sorted_dst[:, a], in_=sorted_src[:, a])
 
         def quantise_feat(g):
             nc.vector.quantize_mx(
@@ -325,11 +335,11 @@ def tile_selsahead_pa_kernel(tc, q, k, feat, conv_w, conv_b, out):
         e0, sum0 = exponentials(s0, shift0)
 
         s1 = new_scores()
-        scores(s1, 1, range(0, 4))
         fill_bank(q_job(2, vector_copy))
+        scores(s1, 1, range(0, 4))
+        fill_bank(q_job(3, vector_copy))
         scores(s1, 1, range(4, 8))
         regroup_feat(2)
-        fill_bank(q_job(3, scalar_copy))
         inv0 = invert(sum0)
         shift1 = row_shift(s1)
         fill_bank(w_job(0, 0, vector_copy))
@@ -348,24 +358,25 @@ def tile_selsahead_pa_kernel(tc, q, k, feat, conv_w, conv_b, out):
 
         s3 = new_scores()
         scores(s3, 3, range(0, 4))
-        quantise_feat(1)
         quantise_e(0, eg0)
+        quantise_feat(1)
         eg1 = turn_e(e1)
         fill_bank(w_job(1, 0, scalar_copy))
         scores(s3, 3, range(4, 8))
         fill_bank(w_job(0, 1, scalar_copy))
-        inv2 = invert(sum2)
-        quantise_e(1, eg1)
         shift3 = row_shift(s3)
+        inv2 = invert(sum2)
         agg0 = aggregate(0)
         e3, sum3 = exponentials(s3, shift3)
         eg2 = turn_e(e2)
         inv_all1 = spread_inv(inv1)
         fill_bank(w_job(1, 1, scalar_copy))
-        grouped0 = divide(agg0, inv_all0)
+        grouped0 = new_grouped()
+        divide(0, agg0, inv_all0, grouped0)
+        quantise_e(1, eg1)
+        divide(1, agg0, inv_all0, grouped0)
         quantise_w(0, 0)
         quantise_agg(0, grouped0)
-        quantise_w(0, 1)
         inv3 = invert(sum3)
         agg1 = aggregate(1)
         quantise_e(2, eg2)
@@ -373,13 +384,18 @@ def tile_selsahead_pa_kernel(tc, q, k, feat, conv_w, conv_b, out):
         inv_all2 = spread_inv(inv2)
         fill_bank(w_job(2, 0, scalar_copy))
         fill_bank(w_job(3, 0, scalar_copy))
-        grouped1 = divide(agg1, inv_all1)
+        grouped1 = new_grouped()
+        for g in range(PASSES):
+            divide(g, agg1, inv_all1, grouped1)
+        quantise_w(0, 1)
         quantise_e(3, eg3)
         quantise_agg(1, grouped1)
         inv_all3 = spread_inv(inv3)
         agg2 = aggregate(2)
         out00 = project(0, 0)
-        grouped2 = divide(agg2, inv_all2)
+        grouped2 = new_grouped()
+        for g in range(PASSES):
+            divide(g, agg2, inv_all2, grouped2)
         quantise_w(1, 0)
         finish(0, 0, residual_sum(0, 0, out00), relu_on_gpsimd)
         quantise_agg(2, grouped2)
@@ -387,7 +403,9 @@ def tile_selsahead_pa_kernel(tc, q, k, feat, conv_w, conv_b, out):
         fill_bank(w_job(3, 1, scalar_copy))
         agg3 = aggregate(3)
         out10 = project(1, 0)
-        grouped3 = divide(agg3, inv_all3)
+        grouped3 = new_grouped()
+        for g in range(PASSES):
+            divide(g, agg3, inv_all3, grouped3)
         out20 = project(2, 0)
         finish(1, 0, residual_sum(1, 0, out10), relu_on_gpsimd)
         quantise_agg(3, grouped3)
@@ -399,9 +417,11 @@ def tile_selsahead_pa_kernel(tc, q, k, feat, conv_w, conv_b, out):
         out11 = project(1, 1)
         finish(3, 0, residual_sum(3, 0, out30), relu_on_scalar)
         out21 = project(2, 1)
-        finish(0, 1, residual_sum(0, 1, out01), relu_on_scalar)
+        finish(0, 1, residual_sum(0, 1, out01), relu_on_gpsimd)
         out31 = project(3, 1)
         finish(1, 1, residual_sum(1, 1, out11), relu_on_scalar)
-        finish(2, 1, residual_sum(2, 1, out21), relu_on_scalar)
+        result21 = residual_sum(2, 1, out21)
+        results31 = [residual_sum(3, 1, out31, piece, 2) for piece in range(2)]
+        finish(2, 1, result21, relu_on_vector)
         for piece in range(2):
-            finish(3, 1, residual_sum(3, 1, out31, piece, 2), relu_on_scalar, piece)
+            finish(3, 1, results31[piece], relu_on_vector, piece)

@@ -101,8 +101,8 @@ def tile_selsahead_pa_kernel(tc, q, k, feat, conv_w, conv_b, out):
         def bias_copy(h, bias_ps):
             nc.scalar.copy(out=bias_all[:, half(h)], in_=bias_ps[:])
 
-        def add_bias_to_feat(j, h):
-            nc.gpsimd.tensor_tensor(
+        def add_bias_to_feat(j, h, engine):
+            engine.tensor_tensor(
                 out=feat_bias[:, j, half(h)], in0=feat_sb[:, j, half(h)], in1=bias_all[:, half(h)], op=ALU.add
             )
 
@@ -277,6 +277,12 @@ def tile_selsahead_pa_kernel(tc, q, k, feat, conv_w, conv_b, out):
             nc.vector.tensor_tensor(out=result[:], in0=out_ps[:, local], in1=feat_bias[:, j, cols], op=ALU.add)
             return result
 
+        def residual_sum_on_gpsimd(j, h, out_ps):
+            result = results.tile([P, BANK], F32, tag="result%d" % BANK, name="result")
+            nc.scalar.copy(out=result[:], in_=out_ps[:])
+            nc.gpsimd.tensor_tensor(out=result[:], in0=result[:], in1=feat_bias[:, j, half(h)], op=ALU.add)
+            return result
+
         def finish(j, h, result, relu, piece=0):
             width = result.shape[1]
             relu(result[:])
@@ -318,18 +324,19 @@ def tile_selsahead_pa_kernel(tc, q, k, feat, conv_w, conv_b, out):
         warm(1)
         fill_bank(k_job(2, scalar_copy))
         fill_bank(k_job(3, vector_copy))
+        s0 = new_scores()
+        first_scores(s0, 0)
         fill_bank(q_job(1, vector_copy))
         bias0 = bias_matmul(0)
         bias1 = bias_matmul(1)
         bias_copy(0, bias0)
         bias_copy(1, bias1)
-        s0 = new_scores()
-        first_scores(s0, 0)
         first_scores(s0, 1)
         regroup_feat(0)
         halves = [(j, h) for j in range(CHUNKS) for h in range(HALVES)]
-        for j, h in halves[:-1]:
-            add_bias_to_feat(j, h)
+        add_bias_to_feat(*halves[0], nc.vector)
+        for j, h in halves[1:-1]:
+            add_bias_to_feat(j, h, nc.gpsimd)
         regroup_feat(1)
         shift0 = row_shift(s0)
         e0, sum0 = exponentials(s0, shift0)
@@ -360,16 +367,16 @@ def tile_selsahead_pa_kernel(tc, q, k, feat, conv_w, conv_b, out):
         scores(s3, 3, range(0, 4))
         quantise_e(0, eg0)
         quantise_feat(1)
+        scores(s3, 3, range(4, 8))
         eg1 = turn_e(e1)
         fill_bank(w_job(1, 0, scalar_copy))
-        scores(s3, 3, range(4, 8))
-        fill_bank(w_job(0, 1, scalar_copy))
         shift3 = row_shift(s3)
         inv2 = invert(sum2)
         agg0 = aggregate(0)
         e3, sum3 = exponentials(s3, shift3)
         eg2 = turn_e(e2)
         inv_all1 = spread_inv(inv1)
+        fill_bank(w_job(0, 1, scalar_copy))
         fill_bank(w_job(1, 1, scalar_copy))
         grouped0 = new_grouped()
         divide(0, agg0, inv_all0, grouped0)
@@ -397,7 +404,7 @@ def tile_selsahead_pa_kernel(tc, q, k, feat, conv_w, conv_b, out):
         for g in range(PASSES):
             divide(g, agg2, inv_all2, grouped2)
         quantise_w(1, 0)
-        finish(0, 0, residual_sum(0, 0, out00), relu_on_gpsimd)
+        finish(0, 0, residual_sum_on_gpsimd(0, 0, out00), relu_on_gpsimd)
         quantise_agg(2, grouped2)
         fill_bank(w_job(2, 1, scalar_copy))
         fill_bank(w_job(3, 1, scalar_copy))
@@ -407,10 +414,10 @@ def tile_selsahead_pa_kernel(tc, q, k, feat, conv_w, conv_b, out):
         for g in range(PASSES):
             divide(g, agg3, inv_all3, grouped3)
         out20 = project(2, 0)
-        finish(1, 0, residual_sum(1, 0, out10), relu_on_gpsimd)
         quantise_agg(3, grouped3)
         quantise_w(1, 1)
-        add_bias_to_feat(*halves[-1])
+        finish(1, 0, residual_sum(1, 0, out10), relu_on_gpsimd)
+        add_bias_to_feat(*halves[-1], nc.gpsimd)
         finish(2, 0, residual_sum(2, 0, out20), relu_on_scalar)
         out30 = project(3, 0)
         out01 = project(0, 1)

@@ -414,8 +414,8 @@ def tile_selsahead_pa_kernel(tc, q, k, feat, conv_w, conv_b, out):
         for g in range(PASSES):
             divide(g, agg3, inv_all3, grouped3)
         out20 = project(2, 0)
-        quantise_agg(3, grouped3)
         quantise_w(1, 1)
+        quantise_agg(3, grouped3)
         finish(1, 0, residual_sum(1, 0, out10), relu_on_gpsimd)
         add_bias_to_feat(*halves[-1], nc.gpsimd)
         finish(2, 0, residual_sum(2, 0, out20), relu_on_scalar)

import math
from contextlib import ExitStack

import concourse.mybir as mybir
from concourse.masks import make_identity

F32 = mybir.dt.float32
BF16 = mybir.dt.bfloat16
U32 = mybir.dt.uint32
U8 = mybir.dt.uint8
FP8X4 = mybir.dt.float8_e4m3fn_x4
ALU = mybir.AluOpType
ACT = mybir.ActivationFunctionType

P = 128
PACK = 4
N_PROP = 512
D = 1024
CHUNKS = N_PROP // P
W_ROWS = D // P
BANK = 512
HALVES = D // BANK
PASSES = D // (P * PACK)
BLOCKS = D // (2 * P)
SCALE = 1.0 / 32.0

FLOPS = 2 * N_PROP * N_PROP * D * 2 + 2 * N_PROP * D * D


def tile_selsahead_pa_kernel(tc, q, k, feat, conv_w, conv_b, out):
    nc = tc.nc
    with ExitStack() as ctx:
        ctx.enter_context(tc.manual_schedule())
        keep = ctx.enter_context(tc.tile_pool(name="keep", bufs=1))
        work = ctx.enter_context(tc.tile_pool(name="work", bufs=CHUNKS))
        results = ctx.enter_context(tc.tile_pool(name="results", bufs=2 * CHUNKS))
        psum_bank = ctx.enter_context(tc.psum_pool(name="psum_bank", bufs=5))
        psum_e = ctx.enter_context(tc.psum_pool(name="psum_e", bufs=1))
        psum_agg = ctx.enter_context(tc.psum_pool(name="psum_agg", bufs=2))

        table_warmer = keep.tile([P, 1], F32)
        nc.vector.memset(table_warmer[:], 0.0)
        ones_f32 = keep.tile([P, P], F32)
        nc.vector.memset(ones_f32[:], 1.0)
        ones_bf16 = keep.tile([P, P], BF16)
        nc.vector.memset(ones_bf16[:], 1.0)
        bias_rows = keep.tile([P, D], BF16)
        nc.vector.memset(bias_rows[:], 0.0)
        ident_f32 = keep.tile([P, P], F32)
        make_identity(nc, ident_f32[:])

        q_view = q.rearrange("(c p i) d -> p c i d", c=2, i=2)
        k_view = k.rearrange("(j p) d -> p j d", j=CHUNKS)
        feat_view = feat.rearrange("(c p i) d -> p c i d", c=2, i=2)
        out_view = out.rearrange("(c p i) d -> p c i d", c=2, i=2)
        w_view = conv_w.rearrange("(r p) d -> p r d", p=P)

        q_sb = keep.tile([P, CHUNKS, D], BF16)
        k_sb = keep.tile([P, CHUNKS, D], BF16)
        feat_sb = keep.tile([P, CHUNKS, D], BF16)
        w_sb = keep.tile([P, W_ROWS, D], BF16)

        nc.scalar.activation(out=table_warmer[:], in_=table_warmer[:], func=ACT.Exp)
        nc.sync.dma_start(out=q_sb[:, 0, :], in_=q_view[:, 0, 0, :])
        for j in range(CHUNKS):
            nc.sync.dma_start(out=k_sb[:, j, :], in_=k_view[:, j, :])
        nc.sync.dma_start(out=bias_rows[0:1, :], in_=conv_b.rearrange("(o d) -> o d", o=1))
        nc.sync.dma_start(out=q_sb[:, 1, :], in_=q_view[:, 0, 1, :])
        for c in range(2):
            nc.sync.dma_start(out=feat_sb[:, 2 * c : 2 * c + 2, :], in_=feat_view[:, c, :, :])
        nc.sync.dma_start(out=q_sb[:, 2:4, :], in_=q_view[:, 1, :, :])
        for r in range(0, W_ROWS, 2):
            nc.sync.dma_start(out=w_sb[:, r : r + 2, :], in_=w_view[:, r : r + 2, :])

        q_t = keep.tile([P, CHUNKS, BLOCKS, P], F32)
        k_t = keep.tile([P, BLOCKS, N_PROP], F32)
        bias_all = keep.tile([P, D], BF16)
        feat_bias = keep.tile([P, CHUNKS, D], F32)
        feat_grouped = keep.tile([P, D, PACK], BF16, align_bytes=64)
        feat_codes = keep.tile([P, D], U32, align_bytes=64)
        feat_scales = keep.tile([P, D], U8, align_bytes=64)
        w_grouped = keep.tile([P, PASSES, D, 2], F32, align_bytes=64)
        w_codes = keep.tile([P, PASSES, D], U32, align_bytes=64)
        w_scales = keep.tile([P, PASSES, D], U8, align_bytes=64)
        e_codes = keep.tile([P, CHUNKS, P], U32, align_bytes=64)
        e_scales = keep.tile([P, CHUNKS, P], U8, align_bytes=64)
        agg_codes = keep.tile([P, CHUNKS, PASSES, P], U32, align_bytes=64)
        agg_scales = keep.tile([P, CHUNKS, PASSES, P], U8, align_bytes=64)

        vector_copy = nc.vector.tensor_copy
        scalar_copy = nc.scalar.copy

        def half(h):
            return slice(h * BANK, (h + 1) * BANK)

        def bias_matmul(h):
            bias_ps = psum_bank.tile([P, BANK], F32, tag="bank", name="bias_ps")
            nc.tensor.matmul(bias_ps[:], lhsT=ones_bf16[:], rhs=bias_rows[:, half(h)], start=True, stop=True)
            return bias_ps

        def bias_copy(h, bias_ps):
            nc.scalar.copy(out=bias_all[:, half(h)], in_=bias_ps[:])

        def add_bias_to_feat(j, h, engine):
            engine.tensor_tensor(
                out=feat_bias[:, j, half(h)], in0=feat_sb[:, j, half(h)], in1=bias_all[:, half(h)], op=ALU.add
            )

        def rows_job(rows, dest, copy):
            words = rows.bitcast(F32)
            sources = [words[:, c * P : (c + 1) * P] for c in range(BLOCKS)]
            return sources, lambda bank: copy(out=dest, in_=bank[:])

        def q_job(j, copy):
            return rows_job(q_sb[:, j, :], q_t[:, j, :, :], copy)

        def k_job(j, copy):
            return rows_job(k_sb[:, j, :], k_t[:, :, j * P : (j + 1) * P], copy)

        def w_job(pair, g, copy):
            sources = [
                w_sb[:, 2 * pair + r, :].bitcast(F32)[:, (2 * g + u) * P : (2 * g + u + 1) * P]
                for u in range(2)
                for r in range(2)
            ]
            dest = w_grouped[:, g, 2 * pair * P : 2 * (pair + 1) * P, :]
            return sources, lambda bank: copy(
                out=dest, in_=bank[:].rearrange("w (u r) c -> w (r c) u", u=2)
            )

        def fill_bank(job):
            sources, empty = job
            bank = psum_bank.tile([P, 4, P], F32, tag="bank", name="t_bank")
            for slot in range(4):
                nc.tensor.transpose(bank[:, slot, :], sources[slot], ident_f32[:])
            empty(bank)

        def new_scores():
            return psum_bank.tile([P, N_PROP], F32, tag="bank", name="s_ps")

        def score_matmul(s_ps, j, m, keys=slice(0, N_PROP)):
            c, i = divmod(m, 2)
            q_pairs = q_t[:, j, c, :].bitcast(BF16).rearrange("w (n i) -> w n i", i=2)
            k_pairs = k_t[:, c, :].bitcast(BF16).rearrange("w (n i) -> w n i", i=2)
            nc.tensor.matmul(
                s_ps[:, keys],
                lhsT=q_pairs[:, :, i],
                rhs=k_pairs[:, keys, i],
                start=(m == 0),
                stop=(m == 2 * BLOCKS - 1),
            )

        def first_scores(s_ps, half_of_keys):
            for m in range(2 * BLOCKS):
                score_matmul(s_ps, 0, m, slice(half_of_keys * 2 * P, (half_of_keys + 1) * 2 * P))

        def scores(s_ps, j, matmuls):
            for m in matmuls:
                score_matmul(s_ps, j, m)

        def row_shift(s_ps):
            scaled = work.tile([P, N_PROP], BF16)
            shift = work.tile([P, 1], F32)
            nc.vector.tensor_scalar(
                out=scaled[:],
                in0=s_ps[:],
                scalar1=-SCALE,
                scalar2=None,
                op0=ALU.mult,
                op1=ALU.min,
                accum_out=shift[:],
            )
            return shift

        def exponentials(s_ps, shift):
            e_sb = work.tile([P, N_PROP], BF16)
            row_sum = work.tile([P, 1], F32)
            nc.scalar.activation(
                out=e_sb[:], in_=s_ps[:], func=ACT.Exp, bias=shift[:], scale=SCALE, accum_out=row_sum[:]
            )
            return e_sb, row_sum

        def invert(row_sum):
            inv_sum = work.tile([P, 1], F32)
            nc.vector.reciprocal(out=inv_sum[:], in_=row_sum[:])
            return inv_sum

        def turn_e(e_sb):
            words = e_sb[:].bitcast(F32)
            e_t = psum_e.tile([P, 2, P], F32)
            for c in range(2):
                nc.tensor.transpose(e_t[:, c, :], words[:, c * P : (c + 1) * P], ident_f32[:])
            e_grouped = work.tile([P, P, 2], F32, align_bytes=64)
            nc.scalar.copy(out=e_grouped[:], in_=e_t[:].rearrange("p c n -> p n c"))
            return e_grouped

        def spread_inv(inv_sum):
            inv_ps = psum_bank.tile([P, P], F32, tag="bank", name="inv_ps")
            nc.tensor.transpose(inv_ps[:], inv_sum[:].to_broadcast([P, P]), ident_f32[:])
            inv_all = work.tile([P, P], F32)
            nc.scalar.copy(out=inv_all[:], in_=inv_ps[:])
            return inv_all

        def quantise_e(j, e_grouped):
            nc.vector.quantize_mx(
                out=e_codes[:, j, :].bitcast(FP8X4),
                scales=e_scales[:, j, :],
                in_=e_grouped[:].rearrange("p n c -> p (n c)").bitcast(BF16),
            )

        def aggregate(j):
            banks = []
            for g in range(PASSES):
                agg_ps = psum_agg.tile([P, PACK, P], F32)
                for t in range(PACK):
                    cols = slice((g * PACK + t) * P, (g * PACK + t + 1) * P)
                    nc.tensor.matmul_mx(
                        out=agg_ps[:, t, :],
                        lhsT=feat_codes[:, cols].bitcast(FP8X4),
                        lhsT_scale=feat_scales[:, cols],
                        rhs=e_codes[:, j, :].bitcast(FP8X4),
                        rhs_scale=e_scales[:, j, :],
                        start=True,
                        stop=True,
                    )
                banks.append(agg_ps)
            return banks

        def new_grouped():
            return work.tile([P, PASSES, P, PACK], BF16, align_bytes=64, name="agg_grouped")

        def divide(g, banks, inv_all, agg_grouped):
            nc.vector.tensor_tensor(
                out=agg_grouped[:, g, :, :],
                in0=banks[g][:].rearrange("w t n -> w n t"),
                in1=inv_all[:].unsqueeze(2).to_broadcast([P, P, PACK]),
                op=ALU.mult,
            )

        def quantise_agg(j, agg_grouped):
            nc.vector.quantize_mx(
                out=agg_codes[:, j, :, :].rearrange("w g n -> w (g n)").bitcast(FP8X4),
                scales=agg_scales[:, j, :, :].rearrange("w g n -> w (g n)"),
                in_=agg_grouped[:].rearrange("w g n t -> w (g n t)"),
            )

        def project(j, h):
            out_ps = psum_bank.tile([P, BANK], F32, tag="bank", name="out_ps")
            for g in range(PASSES):
                nc.tensor.matmul_mx(
                    out=out_ps[:],
                    lhsT=agg_codes[:, j, g, :].bitcast(FP8X4),
                    lhsT_scale=agg_scales[:, j, g, :],
                    rhs=w_codes[:, g, half(h)].bitcast(FP8X4),
                    rhs_scale=w_scales[:, g, half(h)],
                    start=(g == 0),
                    stop=(g == PASSES - 1),
                )
            return out_ps

        def relu_on_gpsimd(result):
            nc.gpsimd.tensor_scalar(
                out=result, in0=result, scalar1=math.inf, scalar2=0.0, op0=ALU.min, op1=ALU.max
            )

        def relu_on_vector(result):
            nc.vector.tensor_scalar_max(out=result, in0=result, scalar1=0.0)

        def relu_on_scalar(result):
            nc.scalar.activation(out=result, in_=result, func=ACT.Relu)

        def residual_sum(j, h, out_ps, piece=0, pieces=1):
            width = BANK // pieces
            local = slice(piece * width, (piece + 1) * width)
            cols = slice(h * BANK + piece * width, h * BANK + (piece + 1) * width)
            result = results.tile([P, width], F32, tag="result%d" % width, name="result")
            nc.vector.tensor_tensor(out=result[:], in0=out_ps[:, local], in1=feat_bias[:, j, cols], op=ALU.add)
            return result

        def residual_sum_on_gpsimd(j, h, out_ps):
            result = results.tile([P, BANK], F32, tag="result%d" % BANK, name="result")
            nc.scalar.copy(out=result[:], in_=out_ps[:])
            nc.gpsimd.tensor_tensor(out=result[:], in0=result[:], in1=feat_bias[:, j, half(h)], op=ALU.add)
            return result

        def finish(j, h, result, relu, piece=0):
            width = result.shape[1]
            relu(result[:])
            cols = slice(h * BANK + piece * width, h * BANK + (piece + 1) * width)
            nc.sync.dma_start(out=out_view[:, j // 2, j % 2, cols], in_=result[:])

        sorted_src = feat_sb[:].rearrange("p j (a w i) -> p a i w j", a=BLOCKS, i=2)
        sorted_dst = feat_grouped[:].rearrange("p (a i w) j -> p a i w j", a=BLOCKS, i=2)

        def regroup_feat(a):
            copy = vector_copy if a == 0 else scalar_copy
            copy(out=sorted_dst[:, a], in_=sorted_src[:, a])

        def quantise_feat(g):
            nc.vector.quantize_mx(
                out=feat_codes[:, half(g)].bitcast(FP8X4),
                scales=feat_scales[:, half(g)],
                in_=feat_grouped[:, half(g), :].rearrange("p c j -> p (c j)"),
            )

        def quantise_w(h, g):
            nc.vector.quantize_mx(
                out=w_codes[:, g, half(h)].bitcast(FP8X4),
                scales=w_scales[:, g, half(h)],
                in_=w_grouped[:, g, half(h), :].rearrange("w c u -> w (c u)").bitcast(BF16),
            )

        warm_ps = psum_e.tile([P, 2, P], F32, name="e_t")

        def warm(repeats):
            for repeat in range(repeats):
                nc.tensor.matmul(warm_ps[:, 0, :], lhsT=ones_f32[:], rhs=ones_f32[:], start=True, stop=True)

        warm(4)
        fill_bank(q_job(0, scalar_copy))
        fill_bank(k_job(0, vector_copy))
        warm(1)
        fill_bank(k_job(1, vector_copy))
        warm(1)
        fill_bank(k_job(2, scalar_copy))
        fill_bank(k_job(3, vector_copy))
        s0 = new_scores()
        first_scores(s0, 0)
        fill_bank(q_job(1, vector_copy))
        bias0 = bias_matmul(0)
        bias1 = bias_matmul(1)
        bias_copy(0, bias0)
        bias_copy(1, bias1)
        first_scores(s0, 1)
        regroup_feat(0)
        halves = [(j, h) for j in range(CHUNKS) for h in range(HALVES)]
        add_bias_to_feat(*halves[0], nc.vector)
        for j, h in halves[1:-1]:
            add_bias_to_feat(j, h, nc.gpsimd)
        regroup_feat(1)
        shift0 = row_shift(s0)
        e0, sum0 = exponentials(s0, shift0)

        s1 = new_scores()
        fill_bank(q_job(2, vector_copy))
        scores(s1, 1, range(0, 4))
        fill_bank(q_job(3, vector_copy))
        scores(s1, 1, range(4, 8))
        regroup_feat(2)
        inv0 = invert(sum0)
        shift1 = row_shift(s1)
        fill_bank(w_job(0, 0, vector_copy))
        e1, sum1 = exponentials(s1, shift1)

        s2 = new_scores()
        scores(s2, 2, range(0, 4))
        quantise_feat(0)
        eg0 = turn_e(e0)
        inv_all0 = spread_inv(inv0)
        regroup_feat(3)
        scores(s2, 2, range(4, 8))
        shift2 = row_shift(s2)
        inv1 = invert(sum1)
        e2, sum2 = exponentials(s2, shift2)

        s3 = new_scores()
        scores(s3, 3, range(0, 4))
        quantise_e(0, eg0)
        quantise_feat(1)
        scores(s3, 3, range(4, 8))
        eg1 = turn_e(e1)
        fill_bank(w_job(1, 0, scalar_copy))
        shift3 = row_shift(s3)
        inv2 = invert(sum2)
        agg0 = aggregate(0)
        e3, sum3 = exponentials(s3, shift3)
        eg2 = turn_e(e2)
        inv_all1 = spread_inv(inv1)
        fill_bank(w_job(0, 1, scalar_copy))
        fill_bank(w_job(1, 1, scalar_copy))
        grouped0 = new_grouped()
        divide(0, agg0, inv_all0, grouped0)
        quantise_e(1, eg1)
        divide(1, agg0, inv_all0, grouped0)
        quantise_w(0, 0)
        quantise_agg(0, grouped0)
        inv3 = invert(sum3)
        agg1 = aggregate(1)
        quantise_e(2, eg2)
        eg3 = turn_e(e3)
        inv_all2 = spread_inv(inv2)
        fill_bank(w_job(2, 0, scalar_copy))
        fill_bank(w_job(3, 0, scalar_copy))
        grouped1 = new_grouped()
        for g in range(PASSES):
            divide(g, agg1, inv_all1, grouped1)
        quantise_w(0, 1)
        quantise_e(3, eg3)
        quantise_agg(1, grouped1)
        inv_all3 = spread_inv(inv3)
        agg2 = aggregate(2)
        out00 = project(0, 0)
        grouped2 = new_grouped()
        for g in range(PASSES):
            divide(g, agg2, inv_all2, grouped2)
        quantise_w(1, 0)
        finish(0, 0, residual_sum_on_gpsimd(0, 0, out00), relu_on_gpsimd)
        quantise_agg(2, grouped2)
        fill_bank(w_job(2, 1, scalar_copy))
        fill_bank(w_job(3, 1, scalar_copy))
        agg3 = aggregate(3)
        out10 = project(1, 0)
        grouped3 = new_grouped()
        for g in range(PASSES):
            divide(g, agg3, inv_all3, grouped3)
        out20 = project(2, 0)
        quantise_w(1, 1)
        quantise_agg(3, grouped3)
        finish(1, 0, residual_sum(1, 0, out10), relu_on_gpsimd)
        add_bias_to_feat(*halves[-1], nc.gpsimd)
        finish(2, 0, residual_sum(2, 0, out20), relu_on_scalar)
        out30 = project(3, 0)
        out01 = project(0, 1)
        out11 = project(1, 1)
        finish(3, 0, residual_sum(3, 0, out30), relu_on_scalar)
        out21 = project(2, 1)
        finish(0, 1, residual_sum(0, 1, out01), relu_on_gpsimd)
        out31 = project(3, 1)
        finish(1, 1, residual_sum(1, 1, out11), relu_on_scalar)
        result21 = residual_sum(2, 1, out21)
        results31 = [residual_sum(3, 1, out31, piece, 2) for piece in range(2)]
        finish(2, 1, result21, relu_on_vector)
        for piece in range(2):
            finish(3, 1, results31[piece], relu_on_vector, piece)
